import numpy as np
import ml_dtypes


def mxq(x, axis, fmt="e4m3"):
    dtype, down = {"e4m3": (ml_dtypes.float8_e4m3fn, 7), "e5m2": (ml_dtypes.float8_e5m2, 14)}[fmt]
    v = np.moveaxis(np.asarray(x, np.float32).astype(ml_dtypes.bfloat16).astype(np.float64), axis, -1)
    blocks = v.reshape(v.shape[:-1] + (-1, 32))
    amax = np.abs(blocks).max(-1, keepdims=True)
    byte = np.maximum(np.where(amax > 0, np.frexp(amax)[1] - 1 + 127, 0) - down, 1)
    scale = np.exp2(byte - 127.0)
    codes = (blocks / scale).astype(np.float32).astype(dtype).astype(np.float64)
    return np.moveaxis((codes * scale).reshape(v.shape), -1, axis)


WIDE = False


def mx_kscale(k):
    if not WIDE:
        return np.ones(k)
    levels = np.array([10, -10, 5, -5, 0])
    a = np.random.permutation(np.resize(levels, k // 512 * 4)).reshape(k // 512, 4)
    idx = np.arange(k)
    return np.exp2(a[idx // 512, idx % 128 // 32])


BF16 = ml_dtypes.bfloat16


def bf(x):
    return np.asarray(x, np.float32).astype(BF16)


def f64(x):
    return np.asarray(x).astype(np.float64)


B, IN, HID, OUT, LAYERS, NG = 1024, 512, 1024, 512, 2, 4
GW = NG * HID
LN_EPS = 1e-5
SIG_MIN = 1e-6


def sigmoid(v):
    return 1.0 / (1.0 + np.exp(-v))


def softplus(v):
    return np.log(1.0 + np.exp(v))


def setup_inputs():
    s = mx_kscale(HID)
    return {
        "h1": bf(np.random.standard_normal((B, HID)) * 0.3 * s),
        "W_ih1": bf(np.random.standard_normal((GW, HID)) * 3.0 / np.sqrt(HID) / s),
        "hh_gates": bf(np.random.standard_normal(GW) * 0.5),
        "b_ih1": bf(np.random.standard_normal(GW) * 0.3),
        "b_hh1": bf(np.random.standard_normal(GW) * 0.3),
        "c_init": bf(np.random.standard_normal(HID)),
        "mu_W": bf(np.random.standard_normal((OUT, HID)) * 3.0 / np.sqrt(HID)),
        "mu_b": bf(np.random.standard_normal(OUT) * 0.3 + 0.3),
        "ln_g": bf(1.0 + 0.1 * np.random.standard_normal(OUT)),
        "ln_b": bf(0.1 * np.random.standard_normal(OUT)),
        "sig_W": bf(np.random.standard_normal((OUT, HID)) * 3.0 / np.sqrt(HID)),
        "sig_b": bf(np.random.standard_normal(OUT) * 0.3),
    }


def reference(h1, W_ih1, hh_gates, b_ih1, b_hh1, c_init, mu_W, mu_b, ln_g, ln_b, sig_W, sig_b):
    gates = (mxq(f64(h1), 1, "e4m3") @ mxq(f64(W_ih1).T, 0, "e4m3")) + f64(hh_gates) + (f64(b_ih1) + f64(b_hh1))
    i, f, g, o = np.split(gates, NG, axis=-1)
    i, f, o = sigmoid(i), sigmoid(f), sigmoid(o)
    g = np.tanh(g)
    c_new = f * f64(c_init) + i * g
    h2 = o * np.tanh(c_new)
    hq = mxq(h2, 1, "e4m3")
    mu_lin = (hq @ mxq(f64(mu_W).T, 0, "e4m3")) + f64(mu_b)
    mean = mu_lin.mean(axis=-1, keepdims=True)
    var = np.square(mu_lin - mean).mean(axis=-1, keepdims=True)
    mu = (mu_lin - mean) * (1.0 / np.sqrt(var + LN_EPS)) * f64(ln_g) + f64(ln_b)
    sigma = softplus((hq @ mxq(f64(sig_W).T, 0, "e4m3")) + f64(sig_b)) + SIG_MIN
    return mu, sigma

@@ -1,0 +1,394 @@
+import math
+from contextlib import ExitStack
+
+import concourse.mybir as mybir
+from concourse.masks import make_identity
+
+FP8X4 = mybir.dt.float8_e4m3fn_x4
+BF16 = mybir.dt.bfloat16
+F32 = mybir.dt.float32
+U32 = mybir.dt.uint32
+U8 = mybir.dt.uint8
+ACT = mybir.ActivationFunctionType
+ALU = mybir.AluOpType
+
+P = 128
+PACK = 4
+K_PASS = P * PACK
+BANK = 512
+
+B, HID, OUT, GATES = 1024, 1024, 512, 4
+PASSES = HID // K_PASS
+ROW_TILES = 4
+ROW_WORDS = HID // 2
+PASS_WORDS = K_PASS // 2
+LOAD_CODES = ROW_TILES * PASSES * P
+B_TILES = B // P
+HALF_TILES = B_TILES // 2
+SLICES = HID // P
+UNITS = 2 * SLICES
+GATE_I, GATE_F, GATE_G, GATE_O = 0, 1, 2, 3
+LN_EPS = 1e-5
+SIG_MIN = 1e-6
+RAW_BUFS = 4
+
+FLOPS = 2 * B * HID * (GATES * HID + 2 * OUT)
+
+BANKS = ROW_TILES * PASSES // 2
+
+
+def stationary_block(bank, x):
+    return bank, x
+
+
+def moving_block(bank, x):
+    return 2 * (bank % 2) + x, bank // 2
+
+
+def split_halves(words, a, c):
+    start = c * PASS_WORDS
+    return [words[:, a, start + u * P : start + (u + 1) * P] for u in range(2)]
+
+
+def alternate_halves(words, a, c):
+    start = c * PASS_WORDS
+    return [words[:, a, start + u : start + PASS_WORDS : 2] for u in range(2)]
+
+
+def tile_rdecommunicationlstm_pb_kernel(
+    tc, h1, W_ih1, hh_gates, b_ih1, b_hh1, c_init, mu_W, mu_b, ln_g, ln_b, sig_W, sig_b, out_0, out_1
+):
+    nc = tc.nc
+    with ExitStack() as ctx:
+        ctx.enter_context(tc.manual_schedule())
+        consts = ctx.enter_context(tc.tile_pool(name="consts", bufs=1))
+        operands = ctx.enter_context(tc.tile_pool(name="operands", bufs=1))
+        raw_pool = ctx.enter_context(tc.tile_pool(name="raw", bufs=RAW_BUFS))
+        stage = ctx.enter_context(tc.tile_pool(name="stage", bufs=2))
+        gate_pool = ctx.enter_context(tc.tile_pool(name="gates", bufs=2))
+        group_pool = ctx.enter_context(tc.tile_pool(name="groups", bufs=2))
+        head_pool = ctx.enter_context(tc.tile_pool(name="heads", bufs=3))
+        small = ctx.enter_context(tc.tile_pool(name="small", bufs=4))
+        psum_gates = ctx.enter_context(tc.psum_pool(name="psum_gates", bufs=4))
+        psum_aux = ctx.enter_context(tc.psum_pool(name="psum_aux", bufs=4))
+
+        bias_rows = consts.tile([P, 3, GATES * SLICES], BF16)
+        for v, vec in enumerate((hh_gates, b_ih1, b_hh1)):
+            nc.scalar.dma_start(
+                out=bias_rows[:, v, :].rearrange("p (s t) -> p s t", t=PACK),
+                in_=vec.rearrange("(s p t) -> p s t", p=P, t=PACK),
+            )
+        cell_rows = consts.tile([P, SLICES], BF16)
+        nc.scalar.dma_start(
+            out=cell_rows[:].rearrange("p (s t) -> p s t", t=PACK),
+            in_=c_init.rearrange("(s p t) -> p s t", p=P, t=PACK),
+        )
+        ident = consts.tile([P, P], F32)
+        make_identity(nc, ident[:])
+        neg_half = consts.tile([P, 1], F32)
+        nc.vector.memset(neg_half[:], -0.5)
+        warm = consts.tile([P, 1], F32)
+        nc.vector.memset(warm[:], 0.0)
+        nc.scalar.activation(out=warm[:], in_=warm[:], func=ACT.Sigmoid)
+
+        gate_bias = consts.tile([P, GATES * SLICES], F32)
+        nc.vector.tensor_tensor(out=gate_bias[:], in0=bias_rows[:, 1, :], in1=bias_rows[:, 2, :], op=ALU.add)
+        nc.vector.tensor_tensor(out=gate_bias[:], in0=gate_bias[:], in1=bias_rows[:, 0, :], op=ALU.add)
+        cell0 = consts.tile([P, SLICES], F32)
+        nc.vector.tensor_copy(out=cell0[:], in_=cell_rows[:])
+
+        row_vectors = consts.tile([P, 4, OUT], BF16)
+        mu_b_rows, ln_g_rows, ln_b_rows, sig_b_rows = [row_vectors[:, v, :] for v in range(4)]
+
+        w_codes = operands.tile([P, SLICES * LOAD_CODES], U32, align_bytes=64)
+        w_scales = operands.tile([P, SLICES * LOAD_CODES], U8, align_bytes=64)
+        h1_codes = operands.tile([P, 2 * LOAD_CODES], U32, align_bytes=64)
+        h1_scales = operands.tile([P, 2 * LOAD_CODES], U8, align_bytes=64)
+        head_codes = operands.tile([P, 2 * LOAD_CODES], U32, align_bytes=64)
+        head_scales = operands.tile([P, 2 * LOAD_CODES], U8, align_bytes=64)
+        h2_codes = operands.tile([P, PASSES * B], U32, align_bytes=64)
+        h2_scales = operands.tile([P, PASSES * B], U8, align_bytes=64)
+
+        h1_rows = h1.rearrange("(p j) k -> p j k", j=B_TILES)
+        w_rows = W_ih1.rearrange("(q g p t) k -> g t p q k", q=GATES, g=PASSES, p=P, t=PACK)
+
+        def source(rows, halves, block, codes, scales, index):
+            cols = slice(index * LOAD_CODES, (index + 1) * LOAD_CODES)
+            return {"rows": rows, "halves": halves, "block": block, "codes": codes[:, cols], "scales": scales[:, cols]}
+
+        def h1_source(half):
+            rows = h1_rows[:, half * HALF_TILES : (half + 1) * HALF_TILES, :]
+            return source(rows, split_halves, moving_block, h1_codes, h1_scales, half)
+
+        def head_source(weights, head):
+            rows = weights.rearrange("(j p) k -> p j k", p=P)
+            return source(rows, alternate_halves, moving_block, head_codes, head_scales, head)
+
+        sources = [h1_source(0)]
+        for s in range(SLICES):
+            sources.append(source(w_rows[s // PACK, s % PACK], split_halves, stationary_block, w_codes, w_scales, s))
+        sources.extend([h1_source(1), head_source(mu_W, 0), head_source(sig_W, 1)])
+        raw_words = {}
+
+        def load_rows(r):
+            raw = raw_pool.tile([P, ROW_TILES * HID], BF16, tag="raw")
+            nc.sync.dma_start(out=raw[:].rearrange("p (a k) -> p a k", a=ROW_TILES), in_=sources[r]["rows"])
+            raw_words[r] = raw[:].bitcast(F32).rearrange("p (a w) -> p a w", a=ROW_TILES)
+            if r == len(sources) - 1:
+                for v, vec in enumerate((mu_b, ln_g, ln_b, sig_b)):
+                    nc.sync.dma_start(out=row_vectors[:, v, :], in_=vec.partition_broadcast(P))
+
+        banks = {}
+        grouped = {}
+
+        def transpose_rows(r):
+            for b in range(BANKS):
+                bank = psum_aux.tile([P, 2, 2, P], F32, tag="aux")
+                for x in range(2):
+                    a, c = sources[r]["block"](b, x)
+                    for u, half in enumerate(sources[r]["halves"](raw_words[r], a, c)):
+                        nc.tensor.transpose(out=bank[:, x, u, :], in_=half, identity=ident[:])
+                banks[(r, b)] = bank
+            group_tile = stage.tile([P, LOAD_CODES * PACK], BF16, tag="grouped", align_bytes=64)
+            grouped[r] = group_tile
+
+        def empty_bank(r, b, copy):
+            words = grouped[r][:].bitcast(F32).rearrange("p (b x r u) -> p b x r u", b=BANKS, x=2, r=P, u=2)
+            copy(out=words[:, b], in_=banks[(r, b)][:].rearrange("p x u r -> p x r u"))
+
+        def quantise_half(r, h):
+            half_codes = LOAD_CODES // 2
+            cols = slice(h * half_codes, (h + 1) * half_codes)
+            nc.vector.quantize_mx(
+                out=sources[r]["codes"][:, cols].bitcast(FP8X4),
+                scales=sources[r]["scales"][:, cols],
+                in_=grouped[r][:, h * half_codes * PACK : (h + 1) * half_codes * PACK],
+            )
+
+        gate_acc = {}
+        gate_out = {}
+        cells = {}
+        groups = {}
+
+        def gate_product(n, q):
+            half, s = divmod(n, SLICES)
+            acc = psum_gates.tile([P, BANK], F32, tag="gate")
+            for c in range(PASSES):
+                w_start = ((s * GATES + q) * PASSES + c) * P
+                x_start = (half * PASSES + c) * BANK
+                nc.tensor.matmul_mx(
+                    out=acc[:],
+                    lhsT=w_codes[:, w_start : w_start + P].bitcast(FP8X4),
+                    lhsT_scale=w_scales[:, w_start : w_start + P],
+                    rhs=h1_codes[:, x_start : x_start + BANK].bitcast(FP8X4),
+                    rhs_scale=h1_scales[:, x_start : x_start + BANK],
+                    start=(c == 0),
+                    stop=(c == PASSES - 1),
+                )
+            gate_acc[(n, q)] = acc
+
+        def gate_function(n, q):
+            s = n % SLICES
+            t = s % PACK
+            if q == GATE_O:
+                if t == 0:
+                    o_group = group_pool.tile([P, PACK, BANK], F32, tag="o", bufs=3)
+                    tanh_group = group_pool.tile([P, PACK, BANK], F32, tag="tanh_c")
+                    groups[n // PACK] = (o_group, tanh_group)
+                value = groups[n // PACK][0][:, t, :]
+            else:
+                gate_tile = gate_pool.tile([P, BANK], F32, tag="gate%d" % q)
+                value = gate_tile[:]
+            col = (q * PASSES + s // PACK) * PACK + t
+            nc.scalar.activation(
+                out=value,
+                in_=gate_acc[(n, q)][:],
+                func=ACT.Tanh if q == GATE_G else ACT.Sigmoid,
+                bias=gate_bias[:, col : col + 1],
+                scale=1.0,
+            )
+            gate_out[(n, q)] = value
+
+        def gate(n, q):
+            gate_function(n, q)
+            if n + 1 < UNITS:
+                gate_product(n + 1, q)
+
+        def cell_update(n):
+            s = n % SLICES
+            input_term = gate_pool.tile([P, BANK], F32, tag="input_term")
+            nc.vector.tensor_tensor(out=input_term[:], in0=gate_out[(n, GATE_I)], in1=gate_out[(n, GATE_G)], op=ALU.mult)
+            cell = gate_pool.tile([P, BANK], F32, tag="cell")
+            nc.vector.scalar_tensor_tensor(
+                out=cell[:], in0=gate_out[(n, GATE_F)], scalar=cell0[:, s : s + 1], in1=input_term[:],
+                op0=ALU.mult, op1=ALU.add,
+            )
+            cells[n] = cell
+
+        def cell_tanh(n):
+            nc.scalar.activation(out=groups[n // PACK][1][:, n % PACK, :], in_=cells[n][:], func=ACT.Tanh)
+
+        hidden = {}
+
+        def hidden_product(grp, jj):
+            o_group, tanh_group = groups[grp]
+            rows = slice(jj * P, (jj + 1) * P)
+            h2_grouped = stage.tile([P, P * PACK], BF16, tag="h2", align_bytes=64)
+            nc.vector.tensor_tensor(
+                out=h2_grouped[:].rearrange("p (x i t) -> p x t i", i=4, t=PACK),
+                in0=o_group[:, :, rows].rearrange("p t (x i) -> p x t i", i=4),
+                in1=tanh_group[:, :, rows].rearrange("p t (x i) -> p x t i", i=4),
+                op=ALU.mult,
+            )
+            hidden[(grp, jj)] = h2_grouped
+
+        def hidden_quantise(grp, jj):
+            half, g = divmod(grp, PASSES)
+            start = g * B + (half * HALF_TILES + jj) * P
+            nc.vector.quantize_mx(
+                out=h2_codes[:, start : start + P].bitcast(FP8X4),
+                scales=h2_scales[:, start : start + P],
+                in_=hidden[(grp, jj)][:],
+            )
+
+        mu_out = out_0.rearrange("(p j) n -> p j n", j=B_TILES)
+        sigma_out = out_1.rearrange("(p j) n -> p j n", j=B_TILES)
+        spread_in = head_pool.tile([P, B_TILES, OUT], F32, tag="spread_in", bufs=1)
+        spread_log = head_pool.tile([P, B_TILES, OUT], F32, tag="spread_log", bufs=1)
+        mean_tiles = {}
+
+        def head_product(j, head):
+            acc = psum_aux.tile([P, BANK], F32, tag="aux")
+            for c in range(PASSES):
+                b_start = c * B + j * P
+                n_start = (head * PASSES + c) * OUT
+                nc.tensor.matmul_mx(
+                    out=acc[:],
+                    lhsT=h2_codes[:, b_start : b_start + P].bitcast(FP8X4),
+                    lhsT_scale=h2_scales[:, b_start : b_start + P],
+                    rhs=head_codes[:, n_start : n_start + OUT].bitcast(FP8X4),
+                    rhs_scale=head_scales[:, n_start : n_start + OUT],
+                    start=(c == 0),
+                    stop=(c == PASSES - 1),
+                )
+            return acc
+
+        def spread_start(j):
+            acc = head_product(j, 1)
+            nc.vector.tensor_tensor(out=spread_in[:, j, :], in0=acc[:], in1=sig_b_rows, op=ALU.add)
+
+        def spread_sigmoid(j):
+            nc.scalar.activation(out=spread_log[:, j, :], in_=spread_in[:, j, :], func=ACT.Abs)
+            nc.scalar.activation(out=spread_log[:, j, :], in_=spread_log[:, j, :], func=ACT.Sigmoid)
+
+        def mean_start(j):
+            acc = head_product(j, 0)
+            mean = head_pool.tile([P, OUT], F32, tag="mean")
+            nc.vector.tensor_tensor(out=mean[:], in0=acc[:], in1=mu_b_rows, op=ALU.add)
+            stats = small.tile([P, 6], F32, tag="stats")
+            nc.vector.bn_stats(out=stats[:], in_=mean[:])
+            mean_var = small.tile([P, 2], F32, tag="mean_var")
+            nc.vector.bn_aggr(out=mean_var[:], in_=stats[:])
+            var_eps = small.tile([P, 1], F32, tag="var_eps")
+            nc.vector.tensor_scalar_add(out=var_eps[:], in0=mean_var[:, 1:2], scalar1=LN_EPS)
+            rstd = small.tile([P, 1], F32, tag="rstd")
+            nc.gpsimd.tensor_tensor(out=rstd[:], in0=var_eps[:], in1=neg_half[:], op=ALU.pow)
+            nc.vector.scalar_tensor_tensor(
+                out=mean[:], in0=mean[:], scalar=mean_var[:, 0:1], in1=ln_g_rows, op0=ALU.subtract, op1=ALU.mult
+            )
+            mean_tiles[j] = (mean, rstd)
+
+        def mean_finish(j):
+            mean, rstd = mean_tiles[j]
+            nc.vector.scalar_tensor_tensor(
+                out=mean[:], in0=mean[:], scalar=rstd[:], in1=ln_b_rows, op0=ALU.mult, op1=ALU.add
+            )
+            nc.sync.dma_start(out=mu_out[:, j, :], in_=mean[:])
+
+        def spread_finish(j):
+            nc.vector.scalar_tensor_tensor(
+                out=spread_in[:, j, :], in0=spread_in[:, j, :], scalar=0.0, in1=spread_log[:, j, :],
+                op0=ALU.max, op1=ALU.subtract,
+            )
+            nc.sync.dma_start(out=sigma_out[:, j, :], in_=spread_in[:, j, :])
+
+        def prepare(r, vector_banks):
+            transpose_rows(r)
+            load_rows(r + RAW_BUFS)
+            for b in range(BANKS):
+                empty_bank(r, b, nc.vector.tensor_copy if b < vector_banks else nc.scalar.copy)
+            for h in range(2):
+                quantise_half(r, h)
+
+        def hidden_piece(k):
+            return k // HALF_TILES, k % HALF_TILES
+
+        for r in range(RAW_BUFS):
+            load_rows(r)
+        prepare(0, BANKS // 2)
+        prepare(1, BANKS // 2)
+        for q in range(GATES):
+            gate_product(0, q)
+        prepare(2, BANKS)
+        transpose_rows(3)
+        load_rows(3 + RAW_BUFS)
+
+        HIDDEN_LAG = PACK + 1
+        PIECES = UNITS
+        FIRST_HEAD = HALF_TILES + HIDDEN_LAG + 1
+        for n in range(UNITS):
+            r = n + 3
+            k = n - HIDDEN_LAG
+            head_j = n - FIRST_HEAD
+            if n > 0:
+                cell_update(n - 1)
+            if 3 < r <= len(sources):
+                quantise_half(r - 1, 1)
+            if r < len(sources):
+                empty_bank(r, 0, nc.vector.tensor_copy)
+                empty_bank(r, 1, nc.vector.tensor_copy)
+            if k >= 0:
+                hidden_product(*hidden_piece(k))
+            if r < len(sources):
+                quantise_half(r, 0)
+            if 0 <= head_j < HALF_TILES:
+                spread_start(head_j)
+                mean_start(head_j)
+            gate(n, GATE_I)
+            gate(n, GATE_G)
+            gate(n, GATE_F)
+            gate(n, GATE_O)
+            if n > 0:
+                cell_tanh(n - 1)
+            if r < len(sources):
+                empty_bank(r, 2, nc.scalar.copy)
+                empty_bank(r, 3, nc.scalar.copy)
+            if r + 1 < len(sources):
+                transpose_rows(r + 1)
+                if r + 1 + RAW_BUFS < len(sources):
+                    load_rows(r + 1 + RAW_BUFS)
+            if 0 <= head_j < HALF_TILES:
+                spread_sigmoid(head_j)
+                mean_finish(head_j)
+            if k >= 0:
+                hidden_quantise(*hidden_piece(k))
+
+        cell_update(UNITS - 1)
+        cell_tanh(UNITS - 1)
+        first_left = UNITS - HIDDEN_LAG
+        hidden_product(*hidden_piece(first_left))
+        for k in range(first_left + 1, PIECES):
+            hidden_product(*hidden_piece(k))
+            hidden_quantise(*hidden_piece(k - 1))
+        hidden_quantise(*hidden_piece(PIECES - 1))
+        for j in range(HALF_TILES, B_TILES):
+            spread_start(j)
+            spread_sigmoid(j)
+        nc.scalar.activation(out=spread_log[:], in_=spread_log[:], func=ACT.Ln, scale=math.exp(-SIG_MIN))
+        for j in range(HALF_TILES, B_TILES):
+            mean_start(j)
+            if j > HALF_TILES:
+                mean_finish(j - 1)
+        mean_finish(B_TILES - 1)
+        for j in range(B_TILES):
+            spread_finish(j)

@@ -92,10 +92,12 @@ def tile_rdecommunicationlstm_pb_kernel(
         nc.scalar.activation(out=warm[:], in_=warm[:], func=ACT.Sigmoid)
 
         gate_bias = consts.tile([P, GATES * SLICES], F32)
-        nc.vector.tensor_tensor(out=gate_bias[:], in0=bias_rows[:, 1, :], in1=bias_rows[:, 2, :], op=ALU.add)
-        nc.vector.tensor_tensor(out=gate_bias[:], in0=gate_bias[:], in1=bias_rows[:, 0, :], op=ALU.add)
         cell0 = consts.tile([P, SLICES], F32)
-        nc.vector.tensor_copy(out=cell0[:], in_=cell_rows[:])
+
+        def sum_biases():
+            nc.vector.tensor_tensor(out=gate_bias[:], in0=bias_rows[:, 1, :], in1=bias_rows[:, 2, :], op=ALU.add)
+            nc.vector.tensor_copy(out=cell0[:], in_=cell_rows[:])
+            nc.vector.tensor_tensor(out=gate_bias[:], in0=gate_bias[:], in1=bias_rows[:, 0, :], op=ALU.add)
 
         row_vectors = consts.tile([P, 4, OUT], BF16)
         mu_b_rows, ln_g_rows, ln_b_rows, sig_b_rows = [row_vectors[:, v, :] for v in range(4)]
@@ -167,6 +169,7 @@ def tile_rdecommunicationlstm_pb_kernel(
 
         gate_acc = {}
         gate_out = {}
+        input_terms = {}
         cells = {}
         groups = {}
 
@@ -214,13 +217,16 @@ def tile_rdecommunicationlstm_pb_kernel(
             if n + 1 < UNITS:
                 gate_product(n + 1, q)
 
-        def cell_update(n):
-            s = n % SLICES
+        def cell_input(n):
             input_term = gate_pool.tile([P, BANK], F32, tag="input_term")
             nc.vector.tensor_tensor(out=input_term[:], in0=gate_out[(n, GATE_I)], in1=gate_out[(n, GATE_G)], op=ALU.mult)
+            input_terms[n] = input_term
+
+        def cell_new(n):
+            s = n % SLICES
             cell = gate_pool.tile([P, BANK], F32, tag="cell")
             nc.vector.scalar_tensor_tensor(
-                out=cell[:], in0=gate_out[(n, GATE_F)], scalar=cell0[:, s : s + 1], in1=input_term[:],
+                out=cell[:], in0=gate_out[(n, GATE_F)], scalar=cell0[:, s : s + 1], in1=input_terms[n][:],
                 op0=ALU.mult, op1=ALU.add,
             )
             cells[n] = cell
@@ -255,6 +261,7 @@ def tile_rdecommunicationlstm_pb_kernel(
         sigma_out = out_1.rearrange("(p j) n -> p j n", j=B_TILES)
         spread_in = head_pool.tile([P, B_TILES, OUT], F32, tag="spread_in", bufs=1)
         spread_log = head_pool.tile([P, B_TILES, OUT], F32, tag="spread_log", bufs=1)
+        head_acc = {}
         mean_tiles = {}
 
         def head_product(j, head):
@@ -271,39 +278,64 @@ def tile_rdecommunicationlstm_pb_kernel(
                     start=(c == 0),
                     stop=(c == PASSES - 1),
                 )
-            return acc
+            head_acc[(j, head)] = acc
 
-        def spread_start(j):
-            acc = head_product(j, 1)
-            nc.vector.tensor_tensor(out=spread_in[:, j, :], in0=acc[:], in1=sig_b_rows, op=ALU.add)
+        def mean_sum(j):
+            mu_lin = head_pool.tile([P, OUT], F32, tag="mu_lin")
+            row_sum = small.tile([P, 1], F32, tag="row_sum")
+            nc.vector.scalar_tensor_tensor(
+                out=mu_lin[:], in0=head_acc[(j, 0)][:], scalar=1.0, in1=mu_b_rows, op0=ALU.mult, op1=ALU.add,
+                accum_out=row_sum[:],
+            )
+            mean_tiles[j] = {"mu_lin": mu_lin, "row_sum": row_sum}
 
-        def spread_sigmoid(j):
-            nc.scalar.activation(out=spread_log[:, j, :], in_=spread_in[:, j, :], func=ACT.Abs)
-            nc.scalar.activation(out=spread_log[:, j, :], in_=spread_log[:, j, :], func=ACT.Sigmoid)
+        def mean_centre(j):
+            neg_mean = small.tile([P, 1], F32, tag="neg_mean")
+            nc.vector.tensor_scalar_mul(out=neg_mean[:], in0=mean_tiles[j]["row_sum"][:], scalar1=-1.0 / OUT)
+            mean_tiles[j]["neg_mean"] = neg_mean
 
-        def mean_start(j):
-            acc = head_product(j, 0)
-            mean = head_pool.tile([P, OUT], F32, tag="mean")
-            nc.vector.tensor_tensor(out=mean[:], in0=acc[:], in1=mu_b_rows, op=ALU.add)
-            stats = small.tile([P, 6], F32, tag="stats")
-            nc.vector.bn_stats(out=stats[:], in_=mean[:])
-            mean_var = small.tile([P, 2], F32, tag="mean_var")
-            nc.vector.bn_aggr(out=mean_var[:], in_=stats[:])
+        def mean_scale(j):
+            scaled = head_pool.tile([P, OUT], F32, tag="scaled")
+            nc.vector.scalar_tensor_tensor(
+                out=scaled[:], in0=mean_tiles[j]["mu_lin"][:], scalar=mean_tiles[j]["neg_mean"][:], in1=ln_g_rows,
+                op0=ALU.add, op1=ALU.mult,
+            )
+            mean_tiles[j]["scaled"] = scaled
+
+        def mean_deviation(j):
+            squares = head_pool.tile([P, OUT], F32, tag="squares", bufs=1)
+            square_sum = small.tile([P, 1], F32, tag="square_sum")
+            nc.scalar.activation(
+                out=squares[:], in_=mean_tiles[j]["mu_lin"][:], func=ACT.Square, bias=mean_tiles[j]["neg_mean"][:],
+                scale=1.0, accum_out=square_sum[:],
+            )
             var_eps = small.tile([P, 1], F32, tag="var_eps")
-            nc.vector.tensor_scalar_add(out=var_eps[:], in0=mean_var[:, 1:2], scalar1=LN_EPS)
+            nc.gpsimd.tensor_scalar(
+                out=var_eps[:], in0=square_sum[:], scalar1=1.0 / OUT, scalar2=LN_EPS, op0=ALU.mult, op1=ALU.add
+            )
             rstd = small.tile([P, 1], F32, tag="rstd")
             nc.gpsimd.tensor_tensor(out=rstd[:], in0=var_eps[:], in1=neg_half[:], op=ALU.pow)
-            nc.vector.scalar_tensor_tensor(
-                out=mean[:], in0=mean[:], scalar=mean_var[:, 0:1], in1=ln_g_rows, op0=ALU.subtract, op1=ALU.mult
-            )
-            mean_tiles[j] = (mean, rstd)
+            mean_tiles[j]["rstd"] = rstd
 
         def mean_finish(j):
-            mean, rstd = mean_tiles[j]
+            scaled = mean_tiles[j]["scaled"]
             nc.vector.scalar_tensor_tensor(
-                out=mean[:], in0=mean[:], scalar=rstd[:], in1=ln_b_rows, op0=ALU.mult, op1=ALU.add
+                out=scaled[:], in0=scaled[:], scalar=mean_tiles[j]["rstd"][:], in1=ln_b_rows, op0=ALU.mult, op1=ALU.add
             )
-            nc.sync.dma_start(out=mu_out[:, j, :], in_=mean[:])
+            nc.sync.dma_start(out=mu_out[:, j, :], in_=scaled[:])
+
+        def spread_sum(j):
+            nc.vector.tensor_tensor(out=spread_in[:, j, :], in0=head_acc[(j, 1)][:], in1=sig_b_rows, op=ALU.add)
+
+        def spread_abs(j):
+            nc.scalar.activation(out=spread_log[:, j, :], in_=spread_in[:, j, :], func=ACT.Abs)
+
+        def spread_sigmoid(j):
+            nc.scalar.activation(out=spread_log[:, j, :], in_=spread_log[:, j, :], func=ACT.Sigmoid)
+
+        def spread_ln(half):
+            tiles = spread_log[:, half * HALF_TILES : (half + 1) * HALF_TILES, :]
+            nc.scalar.activation(out=tiles, in_=tiles, func=ACT.Ln, scale=math.exp(-SIG_MIN))
 
         def spread_finish(j):
             nc.vector.scalar_tensor_tensor(
@@ -320,13 +352,14 @@ def tile_rdecommunicationlstm_pb_kernel(
             for h in range(2):
                 quantise_half(r, h)
 
-        def hidden_piece(k):
+        def piece(k):
             return k // HALF_TILES, k % HALF_TILES
 
         for r in range(RAW_BUFS):
             load_rows(r)
         prepare(0, BANKS // 2)
         prepare(1, BANKS // 2)
+        sum_biases()
         for q in range(GATES):
             gate_product(0, q)
         prepare(2, BANKS)
@@ -335,60 +368,83 @@ def tile_rdecommunicationlstm_pb_kernel(
 
         HIDDEN_LAG = PACK + 1
         PIECES = UNITS
-        FIRST_HEAD = HALF_TILES + HIDDEN_LAG + 1
+        FIRST_HEAD = HALF_TILES + HIDDEN_LAG + 2
         for n in range(UNITS):
             r = n + 3
             k = n - HIDDEN_LAG
-            head_j = n - FIRST_HEAD
-            if n > 0:
-                cell_update(n - 1)
+            j = n - FIRST_HEAD
+            loading = r < len(sources)
+            heads = 0 <= j < HALF_TILES
+            if heads:
+                head_product(j, 0)
+                head_product(j, 1)
             if 3 < r <= len(sources):
                 quantise_half(r - 1, 1)
-            if r < len(sources):
+            if loading:
                 empty_bank(r, 0, nc.vector.tensor_copy)
-                empty_bank(r, 1, nc.vector.tensor_copy)
-            if k >= 0:
-                hidden_product(*hidden_piece(k))
-            if r < len(sources):
-                quantise_half(r, 0)
-            if 0 <= head_j < HALF_TILES:
-                spread_start(head_j)
-                mean_start(head_j)
-            gate(n, GATE_I)
-            gate(n, GATE_G)
-            gate(n, GATE_F)
-            gate(n, GATE_O)
             if n > 0:
-                cell_tanh(n - 1)
-            if r < len(sources):
+                cell_input(n - 1)
+            if loading:
+                empty_bank(r, 1, nc.vector.tensor_copy)
+            if heads:
+                mean_sum(j)
+            if n > 0:
+                cell_new(n - 1)
+            if k >= 0:
+                hidden_product(*piece(k))
+            if heads:
+                mean_centre(j)
+            if loading:
+                quantise_half(r, 0)
+            if heads:
+                spread_sum(j)
+                mean_scale(j)
+            if 0 <= j - 1 < HALF_TILES:
+                mean_finish(j - 1)
+            if k >= 0:
+                hidden_quantise(*piece(k))
+            gate(n, GATE_I)
+            gate(n, GATE_F)
+            gate(n, GATE_G)
+            gate(n, GATE_O)
+            if loading:
                 empty_bank(r, 2, nc.scalar.copy)
                 empty_bank(r, 3, nc.scalar.copy)
+            if n > 0:
+                cell_tanh(n - 1)
+            if heads:
+                spread_abs(j)
+                mean_deviation(j)
+                spread_sigmoid(j)
             if r + 1 < len(sources):
                 transpose_rows(r + 1)
                 if r + 1 + RAW_BUFS < len(sources):
                     load_rows(r + 1 + RAW_BUFS)
-            if 0 <= head_j < HALF_TILES:
-                spread_sigmoid(head_j)
-                mean_finish(head_j)
-            if k >= 0:
-                hidden_quantise(*hidden_piece(k))
 
-        cell_update(UNITS - 1)
-        cell_tanh(UNITS - 1)
         first_left = UNITS - HIDDEN_LAG
-        hidden_product(*hidden_piece(first_left))
+        cell_input(UNITS - 1)
+        hidden_product(*piece(first_left))
+        cell_new(UNITS - 1)
+        cell_tanh(UNITS - 1)
         for k in range(first_left + 1, PIECES):
-            hidden_product(*hidden_piece(k))
-            hidden_quantise(*hidden_piece(k - 1))
-        hidden_quantise(*hidden_piece(PIECES - 1))
-        for j in range(HALF_TILES, B_TILES):
-            spread_start(j)
-            spread_sigmoid(j)
-        nc.scalar.activation(out=spread_log[:], in_=spread_log[:], func=ACT.Ln, scale=math.exp(-SIG_MIN))
-        for j in range(HALF_TILES, B_TILES):
-            mean_start(j)
-            if j > HALF_TILES:
-                mean_finish(j - 1)
-        mean_finish(B_TILES - 1)
+            hidden_product(*piece(k))
+            hidden_quantise(*piece(k - 1))
+        hidden_quantise(*piece(PIECES - 1))
+        for j in range(HALF_TILES, B_TILES + 2):
+            if j < B_TILES:
+                head_product(j, 0)
+                head_product(j, 1)
+                mean_sum(j)
+                spread_sum(j)
+                mean_centre(j)
+                spread_abs(j)
+                mean_deviation(j)
+                spread_sigmoid(j)
+            if HALF_TILES <= j - 1 < B_TILES:
+                mean_scale(j - 1)
+            if HALF_TILES <= j - 2:
+                mean_finish(j - 2)
+        spread_ln(0)
+        spread_ln(1)
         for j in range(B_TILES):
             spread_finish(j)

@@ -295,7 +295,7 @@ def tile_rdecommunicationlstm_pb_kernel(
             mean_tiles[j]["neg_mean"] = neg_mean
 
         def mean_scale(j):
-            scaled = head_pool.tile([P, OUT], F32, tag="scaled")
+            scaled = head_pool.tile([P, OUT], F32, tag="scaled", bufs=4)
             nc.vector.scalar_tensor_tensor(
                 out=scaled[:], in0=mean_tiles[j]["mu_lin"][:], scalar=mean_tiles[j]["neg_mean"][:], in1=ln_g_rows,
                 op0=ALU.add, op1=ALU.mult,
@@ -327,15 +327,14 @@ def tile_rdecommunicationlstm_pb_kernel(
         def spread_sum(j):
             nc.vector.tensor_tensor(out=spread_in[:, j, :], in0=head_acc[(j, 1)][:], in1=sig_b_rows, op=ALU.add)
 
-        def spread_abs(j):
-            nc.scalar.activation(out=spread_log[:, j, :], in_=spread_in[:, j, :], func=ACT.Abs)
+        def spread_abs(tiles):
+            nc.scalar.activation(out=spread_log[:, tiles, :], in_=spread_in[:, tiles, :], func=ACT.Abs)
 
-        def spread_sigmoid(j):
-            nc.scalar.activation(out=spread_log[:, j, :], in_=spread_log[:, j, :], func=ACT.Sigmoid)
+        def spread_sigmoid(tiles):
+            nc.scalar.activation(out=spread_log[:, tiles, :], in_=spread_log[:, tiles, :], func=ACT.Sigmoid)
 
-        def spread_ln(half):
-            tiles = spread_log[:, half * HALF_TILES : (half + 1) * HALF_TILES, :]
-            nc.scalar.activation(out=tiles, in_=tiles, func=ACT.Ln, scale=math.exp(-SIG_MIN))
+        def spread_ln(j):
+            nc.scalar.activation(out=spread_log[:, j, :], in_=spread_log[:, j, :], func=ACT.Ln, scale=math.exp(-SIG_MIN))
 
         def spread_finish(j):
             nc.vector.scalar_tensor_tensor(
@@ -360,9 +359,16 @@ def tile_rdecommunicationlstm_pb_kernel(
         prepare(0, BANKS // 2)
         prepare(1, BANKS // 2)
         sum_biases()
-        for q in range(GATES):
-            gate_product(0, q)
-        prepare(2, BANKS)
+        gate_product(0, GATE_I)
+        gate_product(0, GATE_F)
+        transpose_rows(2)
+        gate_product(0, GATE_G)
+        gate_product(0, GATE_O)
+        load_rows(2 + RAW_BUFS)
+        for b in range(BANKS):
+            empty_bank(2, b, nc.vector.tensor_copy)
+        for h in range(2):
+            quantise_half(2, h)
         transpose_rows(3)
         load_rows(3 + RAW_BUFS)
 
@@ -413,9 +419,7 @@ def tile_rdecommunicationlstm_pb_kernel(
             if n > 0:
                 cell_tanh(n - 1)
             if heads:
-                spread_abs(j)
                 mean_deviation(j)
-                spread_sigmoid(j)
             if r + 1 < len(sources):
                 transpose_rows(r + 1)
                 if r + 1 + RAW_BUFS < len(sources):
@@ -426,6 +430,8 @@ def tile_rdecommunicationlstm_pb_kernel(
         hidden_product(*piece(first_left))
         cell_new(UNITS - 1)
         cell_tanh(UNITS - 1)
+        spread_abs(slice(0, HALF_TILES))
+        spread_sigmoid(slice(0, HALF_TILES))
         for k in range(first_left + 1, PIECES):
             hidden_product(*piece(k))
             hidden_quantise(*piece(k - 1))
@@ -444,7 +450,6 @@ def tile_rdecommunicationlstm_pb_kernel(
                 mean_scale(j - 1)
             if HALF_TILES <= j - 2:
                 mean_finish(j - 2)
-        spread_ln(0)
-        spread_ln(1)
         for j in range(B_TILES):
+            spread_ln(j)
             spread_finish(j)

@@ -20,13 +20,14 @@ BANK = 512
 B, HID, OUT, GATES = 1024, 1024, 512, 4
 PASSES = HID // K_PASS
 ROW_TILES = 4
-ROW_WORDS = HID // 2
 PASS_WORDS = K_PASS // 2
 LOAD_CODES = ROW_TILES * PASSES * P
+BANKS = ROW_TILES * PASSES // 2
 B_TILES = B // P
 HALF_TILES = B_TILES // 2
 SLICES = HID // P
 UNITS = 2 * SLICES
+PIECES = UNITS
 GATE_I, GATE_F, GATE_G, GATE_O = 0, 1, 2, 3
 LN_EPS = 1e-5
 SIG_MIN = 1e-6
@@ -34,7 +35,15 @@ RAW_BUFS = 4
 
 FLOPS = 2 * B * HID * (GATES * HID + 2 * OUT)
 
-BANKS = ROW_TILES * PASSES // 2
+
+def split_planes(words, a, c):
+    start = c * PASS_WORDS
+    return [words[:, a, start + u * P : start + (u + 1) * P] for u in range(2)]
+
+
+def alternate_planes(words, a, c):
+    start = c * PASS_WORDS
+    return [words[:, a, start + u : start + PASS_WORDS : 2] for u in range(2)]
 
 
 def stationary_block(bank, x):
@@ -43,16 +52,6 @@ def stationary_block(bank, x):
 
 def moving_block(bank, x):
     return 2 * (bank % 2) + x, bank // 2
-
-
-def split_halves(words, a, c):
-    start = c * PASS_WORDS
-    return [words[:, a, start + u * P : start + (u + 1) * P] for u in range(2)]
-
-
-def alternate_halves(words, a, c):
-    start = c * PASS_WORDS
-    return [words[:, a, start + u : start + PASS_WORDS : 2] for u in range(2)]
 
 
 def tile_rdecommunicationlstm_pb_kernel(
@@ -69,8 +68,8 @@ def tile_rdecommunicationlstm_pb_kernel(
         group_pool = ctx.enter_context(tc.tile_pool(name="groups", bufs=2))
         head_pool = ctx.enter_context(tc.tile_pool(name="heads", bufs=3))
         small = ctx.enter_context(tc.tile_pool(name="small", bufs=4))
-        psum_gates = ctx.enter_context(tc.psum_pool(name="psum_gates", bufs=4))
-        psum_aux = ctx.enter_context(tc.psum_pool(name="psum_aux", bufs=4))
+        psum_gates = ctx.enter_context(tc.psum_pool(name="psum_gates", bufs=GATES))
+        psum_aux = ctx.enter_context(tc.psum_pool(name="psum_aux", bufs=BANKS))
 
         bias_rows = consts.tile([P, 3, GATES * SLICES], BF16)
         for v, vec in enumerate((hh_gates, b_ih1, b_hh1)):
@@ -114,23 +113,25 @@ def tile_rdecommunicationlstm_pb_kernel(
         h1_rows = h1.rearrange("(p j) k -> p j k", j=B_TILES)
         w_rows = W_ih1.rearrange("(q g p t) k -> g t p q k", q=GATES, g=PASSES, p=P, t=PACK)
 
-        def source(rows, halves, block, codes, scales, index):
+        def source(rows, planes, block, codes, scales, index):
             cols = slice(index * LOAD_CODES, (index + 1) * LOAD_CODES)
-            return {"rows": rows, "halves": halves, "block": block, "codes": codes[:, cols], "scales": scales[:, cols]}
+            return {"rows": rows, "planes": planes, "block": block, "codes": codes[:, cols], "scales": scales[:, cols]}
 
         def h1_source(half):
             rows = h1_rows[:, half * HALF_TILES : (half + 1) * HALF_TILES, :]
-            return source(rows, split_halves, moving_block, h1_codes, h1_scales, half)
+            return source(rows, split_planes, moving_block, h1_codes, h1_scales, half)
 
         def head_source(weights, head):
             rows = weights.rearrange("(j p) k -> p j k", p=P)
-            return source(rows, alternate_halves, moving_block, head_codes, head_scales, head)
+            return source(rows, alternate_planes, moving_block, head_codes, head_scales, head)
 
         sources = [h1_source(0)]
         for s in range(SLICES):
-            sources.append(source(w_rows[s // PACK, s % PACK], split_halves, stationary_block, w_codes, w_scales, s))
+            sources.append(source(w_rows[s // PACK, s % PACK], split_planes, stationary_block, w_codes, w_scales, s))
         sources.extend([h1_source(1), head_source(mu_W, 0), head_source(sig_W, 1)])
         raw_words = {}
+        banks = {}
+        grouped = {}
 
         def load_rows(r):
             raw = raw_pool.tile([P, ROW_TILES * HID], BF16, tag="raw")
@@ -140,16 +141,13 @@ def tile_rdecommunicationlstm_pb_kernel(
                 for v, vec in enumerate((mu_b, ln_g, ln_b, sig_b)):
                     nc.sync.dma_start(out=row_vectors[:, v, :], in_=vec.partition_broadcast(P))
 
-        banks = {}
-        grouped = {}
-
         def transpose_rows(r):
             for b in range(BANKS):
                 bank = psum_aux.tile([P, 2, 2, P], F32, tag="aux")
                 for x in range(2):
                     a, c = sources[r]["block"](b, x)
-                    for u, half in enumerate(sources[r]["halves"](raw_words[r], a, c)):
-                        nc.tensor.transpose(out=bank[:, x, u, :], in_=half, identity=ident[:])
+                    for u, plane in enumerate(sources[r]["planes"](raw_words[r], a, c)):
+                        nc.tensor.transpose(out=bank[:, x, u, :], in_=plane, identity=ident[:])
                 banks[(r, b)] = bank
             group_tile = stage.tile([P, LOAD_CODES * PACK], BF16, tag="grouped", align_bytes=64)
             grouped[r] = group_tile
@@ -172,6 +170,7 @@ def tile_rdecommunicationlstm_pb_kernel(
         input_terms = {}
         cells = {}
         groups = {}
+        hidden = {}
 
         def gate_product(n, q):
             half, s = divmod(n, SLICES)
@@ -234,12 +233,10 @@ def tile_rdecommunicationlstm_pb_kernel(
         def cell_tanh(n):
             nc.scalar.activation(out=groups[n // PACK][1][:, n % PACK, :], in_=cells[n][:], func=ACT.Tanh)
 
-        hidden = {}
-
         def hidden_product(grp, jj):
             o_group, tanh_group = groups[grp]
             rows = slice(jj * P, (jj + 1) * P)
-            h2_grouped = stage.tile([P, P * PACK], BF16, tag="h2", align_bytes=64)
+            h2_grouped = stage.tile([P, P * PACK], BF16, tag="h2", align_bytes=64, bufs=3)
             nc.vector.tensor_tensor(
                 out=h2_grouped[:].rearrange("p (x i t) -> p x t i", i=4, t=PACK),
                 in0=o_group[:, :, rows].rearrange("p t (x i) -> p x t i", i=4),
@@ -343,21 +340,18 @@ def tile_rdecommunicationlstm_pb_kernel(
             )
             nc.sync.dma_start(out=sigma_out[:, j, :], in_=spread_in[:, j, :])
 
-        def prepare(r, vector_banks):
-            transpose_rows(r)
-            load_rows(r + RAW_BUFS)
-            for b in range(BANKS):
-                empty_bank(r, b, nc.vector.tensor_copy if b < vector_banks else nc.scalar.copy)
-            for h in range(2):
-                quantise_half(r, h)
-
         def piece(k):
             return k // HALF_TILES, k % HALF_TILES
 
         for r in range(RAW_BUFS):
             load_rows(r)
-        prepare(0, BANKS // 2)
-        prepare(1, BANKS // 2)
+        for r in range(2):
+            transpose_rows(r)
+            load_rows(r + RAW_BUFS)
+            for b in range(BANKS):
+                empty_bank(r, b, nc.scalar.copy)
+            for h in range(2):
+                quantise_half(r, h)
         sum_biases()
         gate_product(0, GATE_I)
         gate_product(0, GATE_F)
@@ -373,8 +367,7 @@ def tile_rdecommunicationlstm_pb_kernel(
         load_rows(3 + RAW_BUFS)
 
         HIDDEN_LAG = PACK + 1
-        PIECES = UNITS
-        FIRST_HEAD = HALF_TILES + HIDDEN_LAG + 2
+        FIRST_HEAD = HALF_TILES + HIDDEN_LAG + 1
         for n in range(UNITS):
             r = n + 3
             k = n - HIDDEN_LAG
@@ -404,15 +397,14 @@ def tile_rdecommunicationlstm_pb_kernel(
                 quantise_half(r, 0)
             if heads:
                 spread_sum(j)
+            if k >= 0:
+                hidden_quantise(*piece(k))
+            if heads:
                 mean_scale(j)
             if 0 <= j - 1 < HALF_TILES:
                 mean_finish(j - 1)
-            if k >= 0:
-                hidden_quantise(*piece(k))
-            gate(n, GATE_I)
-            gate(n, GATE_F)
-            gate(n, GATE_G)
-            gate(n, GATE_O)
+            for q in range(GATES):
+                gate(n, q)
             if loading:
                 empty_bank(r, 2, nc.scalar.copy)
                 empty_bank(r, 3, nc.scalar.copy)
@@ -425,13 +417,13 @@ def tile_rdecommunicationlstm_pb_kernel(
                 if r + 1 + RAW_BUFS < len(sources):
                     load_rows(r + 1 + RAW_BUFS)
 
-        first_left = UNITS - HIDDEN_LAG
         cell_input(UNITS - 1)
-        hidden_product(*piece(first_left))
         cell_new(UNITS - 1)
         cell_tanh(UNITS - 1)
         spread_abs(slice(0, HALF_TILES))
         spread_sigmoid(slice(0, HALF_TILES))
+        first_left = UNITS - HIDDEN_LAG
+        hidden_product(*piece(first_left))
         for k in range(first_left + 1, PIECES):
             hidden_product(*piece(k))
             hidden_quantise(*piece(k - 1))

@@ -32,6 +32,7 @@ GATE_I, GATE_F, GATE_G, GATE_O = 0, 1, 2, 3
 LN_EPS = 1e-5
 SIG_MIN = 1e-6
 RAW_BUFS = 4
+RUN = 4
 
 FLOPS = 2 * B * HID * (GATES * HID + 2 * OUT)
 
@@ -46,12 +47,12 @@ def alternate_planes(words, a, c):
     return [words[:, a, start + u : start + PASS_WORDS : 2] for u in range(2)]
 
 
-def stationary_block(bank, x):
-    return bank, x
+def stationary_block(bank, d):
+    return bank, d
 
 
-def moving_block(bank, x):
-    return 2 * (bank % 2) + x, bank // 2
+def moving_block(bank, d):
+    return 2 * (bank % 2) + d, bank // 2
 
 
 def tile_rdecommunicationlstm_pb_kernel(
@@ -71,17 +72,6 @@ def tile_rdecommunicationlstm_pb_kernel(
         psum_gates = ctx.enter_context(tc.psum_pool(name="psum_gates", bufs=GATES))
         psum_aux = ctx.enter_context(tc.psum_pool(name="psum_aux", bufs=BANKS))
 
-        bias_rows = consts.tile([P, 3, GATES * SLICES], BF16)
-        for v, vec in enumerate((hh_gates, b_ih1, b_hh1)):
-            nc.scalar.dma_start(
-                out=bias_rows[:, v, :].rearrange("p (s t) -> p s t", t=PACK),
-                in_=vec.rearrange("(s p t) -> p s t", p=P, t=PACK),
-            )
-        cell_rows = consts.tile([P, SLICES], BF16)
-        nc.scalar.dma_start(
-            out=cell_rows[:].rearrange("p (s t) -> p s t", t=PACK),
-            in_=c_init.rearrange("(s p t) -> p s t", p=P, t=PACK),
-        )
         ident = consts.tile([P, P], F32)
         make_identity(nc, ident[:])
         neg_half = consts.tile([P, 1], F32)
@@ -90,13 +80,37 @@ def tile_rdecommunicationlstm_pb_kernel(
         nc.vector.memset(warm[:], 0.0)
         nc.scalar.activation(out=warm[:], in_=warm[:], func=ACT.Sigmoid)
 
-        gate_bias = consts.tile([P, GATES * SLICES], F32)
+        VECTOR_BLOCKS = GATES * PASSES
+        VECTOR_ROWS = 3 * VECTOR_BLOCKS + PASSES
+        BIAS_COLS = VECTOR_BLOCKS * PACK
+        vector_rows = consts.tile([P, K_PASS], BF16)
+        nc.vector.memset(vector_rows[:], 0.0)
+        vector_cols = consts.tile([P, VECTOR_ROWS * PACK], BF16)
+        gate_bias = consts.tile([P, BIAS_COLS], F32)
         cell0 = consts.tile([P, SLICES], F32)
 
-        def sum_biases():
-            nc.vector.tensor_tensor(out=gate_bias[:], in0=bias_rows[:, 1, :], in1=bias_rows[:, 2, :], op=ALU.add)
-            nc.vector.tensor_copy(out=cell0[:], in_=cell_rows[:])
-            nc.vector.tensor_tensor(out=gate_bias[:], in0=gate_bias[:], in1=bias_rows[:, 0, :], op=ALU.add)
+        def load_vectors():
+            for v, vec in enumerate((hh_gates, b_ih1, b_hh1)):
+                nc.sync.dma_start(
+                    out=vector_rows[v * VECTOR_BLOCKS : (v + 1) * VECTOR_BLOCKS, :],
+                    in_=vec.rearrange("(blk i) -> blk i", i=K_PASS),
+                )
+            nc.sync.dma_start(
+                out=vector_rows[3 * VECTOR_BLOCKS : VECTOR_ROWS, :], in_=c_init.rearrange("(blk i) -> blk i", i=K_PASS)
+            )
+
+        def turn_vectors():
+            vector_bank = psum_aux.tile([P, 2, P], F32, tag="aux")
+            for u in range(2):
+                nc.tensor.transpose(out=vector_bank[:, u, :], in_=vector_rows[:].bitcast(F32)[:, u::2], identity=ident[:])
+            nc.vector.tensor_copy(
+                out=vector_cols[:].bitcast(F32).rearrange("p (row u) -> p row u", u=2),
+                in_=vector_bank[:, :, :VECTOR_ROWS].rearrange("p u row -> p row u"),
+            )
+            hh_cols, ih_cols, bhh_cols = [vector_cols[:, v * BIAS_COLS : (v + 1) * BIAS_COLS] for v in range(3)]
+            nc.vector.tensor_tensor(out=gate_bias[:], in0=ih_cols, in1=bhh_cols, op=ALU.add)
+            nc.vector.tensor_copy(out=cell0[:], in_=vector_cols[:, 3 * BIAS_COLS :])
+            nc.vector.tensor_tensor(out=gate_bias[:], in0=gate_bias[:], in1=hh_cols, op=ALU.add)
 
         row_vectors = consts.tile([P, 4, OUT], BF16)
         mu_b_rows, ln_g_rows, ln_b_rows, sig_b_rows = [row_vectors[:, v, :] for v in range(4)]
@@ -135,7 +149,9 @@ def tile_rdecommunicationlstm_pb_kernel(
 
         def load_rows(r):
             raw = raw_pool.tile([P, ROW_TILES * HID], BF16, tag="raw")
-            nc.sync.dma_start(out=raw[:].rearrange("p (a k) -> p a k", a=ROW_TILES), in_=sources[r]["rows"])
+            row_tiles = raw[:].rearrange("p (a k) -> p a k", a=ROW_TILES)
+            for pair in (slice(0, ROW_TILES // 2), slice(ROW_TILES // 2, ROW_TILES)):
+                nc.sync.dma_start(out=row_tiles[:, pair, :], in_=sources[r]["rows"][:, pair, :])
             raw_words[r] = raw[:].bitcast(F32).rearrange("p (a w) -> p a w", a=ROW_TILES)
             if r == len(sources) - 1:
                 for v, vec in enumerate((mu_b, ln_g, ln_b, sig_b)):
@@ -144,17 +160,17 @@ def tile_rdecommunicationlstm_pb_kernel(
         def transpose_rows(r):
             for b in range(BANKS):
                 bank = psum_aux.tile([P, 2, 2, P], F32, tag="aux")
-                for x in range(2):
-                    a, c = sources[r]["block"](b, x)
+                for d in range(2):
+                    a, c = sources[r]["block"](b, d)
                     for u, plane in enumerate(sources[r]["planes"](raw_words[r], a, c)):
-                        nc.tensor.transpose(out=bank[:, x, u, :], in_=plane, identity=ident[:])
+                        nc.tensor.transpose(out=bank[:, d, u, :], in_=plane, identity=ident[:])
                 banks[(r, b)] = bank
             group_tile = stage.tile([P, LOAD_CODES * PACK], BF16, tag="grouped", align_bytes=64)
             grouped[r] = group_tile
 
         def empty_bank(r, b, copy):
-            words = grouped[r][:].bitcast(F32).rearrange("p (b x r u) -> p b x r u", b=BANKS, x=2, r=P, u=2)
-            copy(out=words[:, b], in_=banks[(r, b)][:].rearrange("p x u r -> p x r u"))
+            words = grouped[r][:].bitcast(F32).rearrange("p (b d row u) -> p b d row u", b=BANKS, d=2, row=P, u=2)
+            copy(out=words[:, b], in_=banks[(r, b)][:].rearrange("p d u row -> p d row u"))
 
         def quantise_half(r, h):
             half_codes = LOAD_CODES // 2
@@ -235,12 +251,12 @@ def tile_rdecommunicationlstm_pb_kernel(
 
         def hidden_product(grp, jj):
             o_group, tanh_group = groups[grp]
-            rows = slice(jj * P, (jj + 1) * P)
+            batch_rows = slice(jj * P, (jj + 1) * P)
             h2_grouped = stage.tile([P, P * PACK], BF16, tag="h2", align_bytes=64, bufs=3)
             nc.vector.tensor_tensor(
-                out=h2_grouped[:].rearrange("p (x i t) -> p x t i", i=4, t=PACK),
-                in0=o_group[:, :, rows].rearrange("p t (x i) -> p x t i", i=4),
-                in1=tanh_group[:, :, rows].rearrange("p t (x i) -> p x t i", i=4),
+                out=h2_grouped[:].rearrange("p (run i t) -> p run t i", i=RUN, t=PACK),
+                in0=o_group[:, :, batch_rows].rearrange("p t (run i) -> p run t i", i=RUN),
+                in1=tanh_group[:, :, batch_rows].rearrange("p t (run i) -> p run t i", i=RUN),
                 op=ALU.mult,
             )
             hidden[(grp, jj)] = h2_grouped
@@ -254,8 +270,8 @@ def tile_rdecommunicationlstm_pb_kernel(
                 in_=hidden[(grp, jj)][:],
             )
 
-        mu_out = out_0.rearrange("(p j) n -> p j n", j=B_TILES)
-        sigma_out = out_1.rearrange("(p j) n -> p j n", j=B_TILES)
+        mu_out = out_0.rearrange("(p j) col -> p j col", j=B_TILES)
+        sigma_out = out_1.rearrange("(p j) col -> p j col", j=B_TILES)
         spread_in = head_pool.tile([P, B_TILES, OUT], F32, tag="spread_in", bufs=1)
         spread_log = head_pool.tile([P, B_TILES, OUT], F32, tag="spread_log", bufs=1)
         head_acc = {}
@@ -265,13 +281,13 @@ def tile_rdecommunicationlstm_pb_kernel(
             acc = psum_aux.tile([P, BANK], F32, tag="aux")
             for c in range(PASSES):
                 b_start = c * B + j * P
-                n_start = (head * PASSES + c) * OUT
+                col_start = (head * PASSES + c) * OUT
                 nc.tensor.matmul_mx(
                     out=acc[:],
                     lhsT=h2_codes[:, b_start : b_start + P].bitcast(FP8X4),
                     lhsT_scale=h2_scales[:, b_start : b_start + P],
-                    rhs=head_codes[:, n_start : n_start + OUT].bitcast(FP8X4),
-                    rhs_scale=head_scales[:, n_start : n_start + OUT],
+                    rhs=head_codes[:, col_start : col_start + OUT].bitcast(FP8X4),
+                    rhs_scale=head_scales[:, col_start : col_start + OUT],
                     start=(c == 0),
                     stop=(c == PASSES - 1),
                 )
@@ -340,10 +356,12 @@ def tile_rdecommunicationlstm_pb_kernel(
             )
             nc.sync.dma_start(out=sigma_out[:, j, :], in_=spread_in[:, j, :])
 
-        def piece(k):
-            return k // HALF_TILES, k % HALF_TILES
+        def piece(m):
+            return m // HALF_TILES, m % HALF_TILES
 
-        for r in range(RAW_BUFS):
+        load_rows(0)
+        load_vectors()
+        for r in range(1, RAW_BUFS):
             load_rows(r)
         for r in range(2):
             transpose_rows(r)
@@ -352,7 +370,8 @@ def tile_rdecommunicationlstm_pb_kernel(
                 empty_bank(r, b, nc.scalar.copy)
             for h in range(2):
                 quantise_half(r, h)
-        sum_biases()
+            if r == 0:
+                turn_vectors()
         gate_product(0, GATE_I)
         gate_product(0, GATE_F)
         transpose_rows(2)
@@ -370,7 +389,7 @@ def tile_rdecommunicationlstm_pb_kernel(
         FIRST_HEAD = HALF_TILES + HIDDEN_LAG + 1
         for n in range(UNITS):
             r = n + 3
-            k = n - HIDDEN_LAG
+            m = n - HIDDEN_LAG
             j = n - FIRST_HEAD
             loading = r < len(sources)
             heads = 0 <= j < HALF_TILES
@@ -389,16 +408,16 @@ def tile_rdecommunicationlstm_pb_kernel(
                 mean_sum(j)
             if n > 0:
                 cell_new(n - 1)
-            if k >= 0:
-                hidden_product(*piece(k))
+            if m >= 0:
+                hidden_product(*piece(m))
             if heads:
                 mean_centre(j)
             if loading:
                 quantise_half(r, 0)
             if heads:
                 spread_sum(j)
-            if k >= 0:
-                hidden_quantise(*piece(k))
+            if m >= 0:
+                hidden_quantise(*piece(m))
             if heads:
                 mean_scale(j)
             if 0 <= j - 1 < HALF_TILES:
@@ -424,9 +443,9 @@ def tile_rdecommunicationlstm_pb_kernel(
         spread_sigmoid(slice(0, HALF_TILES))
         first_left = UNITS - HIDDEN_LAG
         hidden_product(*piece(first_left))
-        for k in range(first_left + 1, PIECES):
-            hidden_product(*piece(k))
-            hidden_quantise(*piece(k - 1))
+        for m in range(first_left + 1, PIECES):
+            hidden_product(*piece(m))
+            hidden_quantise(*piece(m - 1))
         hidden_quantise(*piece(PIECES - 1))
         for j in range(HALF_TILES, B_TILES + 2):
             if j < B_TILES:

@@ -31,6 +31,8 @@ PIECES = UNITS
 GATE_I, GATE_F, GATE_G, GATE_O = 0, 1, 2, 3
 LN_EPS = 1e-5
 SIG_MIN = 1e-6
+TINY = 2.0**-100
+WARM_START = 6
 RAW_BUFS = 4
 RUN = 4
 
@@ -74,8 +76,12 @@ def tile_rdecommunicationlstm_pb_kernel(
 
         ident = consts.tile([P, P], F32)
         make_identity(nc, ident[:])
+        zeros = consts.tile([P, BANK], BF16)
+        nc.vector.memset(zeros[:], 0.0)
         neg_half = consts.tile([P, 1], F32)
         nc.vector.memset(neg_half[:], -0.5)
+        tiny = consts.tile([P, 1], F32)
+        nc.vector.memset(tiny[:], TINY)
         warm = consts.tile([P, 1], F32)
         nc.vector.memset(warm[:], 0.0)
         nc.scalar.activation(out=warm[:], in_=warm[:], func=ACT.Sigmoid)
@@ -156,6 +162,11 @@ def tile_rdecommunicationlstm_pb_kernel(
             if r == len(sources) - 1:
                 for v, vec in enumerate((mu_b, ln_g, ln_b, sig_b)):
                     nc.sync.dma_start(out=row_vectors[:, v, :], in_=vec.partition_broadcast(P))
+
+        def keep_warm(count):
+            for turn in range(count):
+                idle = psum_gates.tile([P, BANK], F32, tag="gate")
+                nc.tensor.matmul(out=idle[:], lhsT=zeros[:, :P], rhs=zeros[:], start=True, stop=True)
 
         def transpose_rows(r):
             for b in range(BANKS):
@@ -340,19 +351,18 @@ def tile_rdecommunicationlstm_pb_kernel(
         def spread_sum(j):
             nc.vector.tensor_tensor(out=spread_in[:, j, :], in0=head_acc[(j, 1)][:], in1=sig_b_rows, op=ALU.add)
 
-        def spread_abs(tiles):
-            nc.scalar.activation(out=spread_log[:, tiles, :], in_=spread_in[:, tiles, :], func=ACT.Abs)
-
         def spread_sigmoid(tiles):
-            nc.scalar.activation(out=spread_log[:, tiles, :], in_=spread_log[:, tiles, :], func=ACT.Sigmoid)
+            nc.scalar.activation(out=spread_log[:, tiles, :], in_=spread_in[:, tiles, :], func=ACT.Sigmoid, scale=-1.0)
 
         def spread_ln(j):
-            nc.scalar.activation(out=spread_log[:, j, :], in_=spread_log[:, j, :], func=ACT.Ln, scale=math.exp(-SIG_MIN))
+            nc.scalar.activation(
+                out=spread_log[:, j, :], in_=spread_log[:, j, :], func=ACT.Ln, bias=tiny[:], scale=math.exp(-SIG_MIN)
+            )
 
         def spread_finish(j):
             nc.vector.scalar_tensor_tensor(
-                out=spread_in[:, j, :], in0=spread_in[:, j, :], scalar=0.0, in1=spread_log[:, j, :],
-                op0=ALU.max, op1=ALU.subtract,
+                out=spread_in[:, j, :], in0=spread_log[:, j, :], scalar=-1.0, in1=spread_in[:, j, :],
+                op0=ALU.mult, op1=ALU.max,
             )
             nc.sync.dma_start(out=sigma_out[:, j, :], in_=spread_in[:, j, :])
 
@@ -363,6 +373,7 @@ def tile_rdecommunicationlstm_pb_kernel(
         load_vectors()
         for r in range(1, RAW_BUFS):
             load_rows(r)
+        keep_warm(WARM_START)
         for r in range(2):
             transpose_rows(r)
             load_rows(r + RAW_BUFS)
@@ -396,12 +407,14 @@ def tile_rdecommunicationlstm_pb_kernel(
             if heads:
                 head_product(j, 0)
                 head_product(j, 1)
-            if 3 < r <= len(sources):
-                quantise_half(r - 1, 1)
-            if loading:
-                empty_bank(r, 0, nc.vector.tensor_copy)
             if n > 0:
                 cell_input(n - 1)
+            if 3 < r <= len(sources):
+                quantise_half(r - 1, 1)
+            if m >= 0:
+                hidden_product(*piece(m))
+            if loading:
+                empty_bank(r, 0, nc.vector.tensor_copy)
             if loading:
                 empty_bank(r, 1, nc.vector.tensor_copy)
             if heads:
@@ -409,15 +422,13 @@ def tile_rdecommunicationlstm_pb_kernel(
             if n > 0:
                 cell_new(n - 1)
             if m >= 0:
-                hidden_product(*piece(m))
+                hidden_quantise(*piece(m))
             if heads:
                 mean_centre(j)
             if loading:
                 quantise_half(r, 0)
             if heads:
                 spread_sum(j)
-            if m >= 0:
-                hidden_quantise(*piece(m))
             if heads:
                 mean_scale(j)
             if 0 <= j - 1 < HALF_TILES:
@@ -439,7 +450,6 @@ def tile_rdecommunicationlstm_pb_kernel(
         cell_input(UNITS - 1)
         cell_new(UNITS - 1)
         cell_tanh(UNITS - 1)
-        spread_abs(slice(0, HALF_TILES))
         spread_sigmoid(slice(0, HALF_TILES))
         first_left = UNITS - HIDDEN_LAG
         hidden_product(*piece(first_left))
@@ -454,7 +464,6 @@ def tile_rdecommunicationlstm_pb_kernel(
                 mean_sum(j)
                 spread_sum(j)
                 mean_centre(j)
-                spread_abs(j)
                 mean_deviation(j)
                 spread_sigmoid(j)
             if HALF_TILES <= j - 1 < B_TILES:

@@ -24,10 +24,10 @@ PASS_WORDS = K_PASS // 2
 LOAD_CODES = ROW_TILES * PASSES * P
 BANKS = ROW_TILES * PASSES // 2
 B_TILES = B // P
-HALF_TILES = B_TILES // 2
 SLICES = HID // P
-UNITS = 2 * SLICES
-PIECES = UNITS
+PARTS = (4, 4)
+PART_START = [sum(PARTS[:part]) for part in range(len(PARTS))]
+UNITS = len(PARTS) * SLICES
 GATE_I, GATE_F, GATE_G, GATE_O = 0, 1, 2, 3
 LN_EPS = 1e-5
 SIG_MIN = 1e-6
@@ -49,12 +49,13 @@ def alternate_planes(words, a, c):
     return [words[:, a, start + u : start + PASS_WORDS : 2] for u in range(2)]
 
 
-def stationary_block(bank, d):
+def stationary_block(tiles, bank, d):
     return bank, d
 
 
-def moving_block(bank, d):
-    return 2 * (bank % 2) + d, bank // 2
+def moving_block(tiles, bank, d):
+    c, a = divmod(2 * bank + d, tiles)
+    return a, c
 
 
 def tile_rdecommunicationlstm_pb_kernel(
@@ -123,8 +124,8 @@ def tile_rdecommunicationlstm_pb_kernel(
 
         w_codes = operands.tile([P, SLICES * LOAD_CODES], U32, align_bytes=64)
         w_scales = operands.tile([P, SLICES * LOAD_CODES], U8, align_bytes=64)
-        h1_codes = operands.tile([P, 2 * LOAD_CODES], U32, align_bytes=64)
-        h1_scales = operands.tile([P, 2 * LOAD_CODES], U8, align_bytes=64)
+        h1_codes = operands.tile([P, PASSES * B], U32, align_bytes=64)
+        h1_scales = operands.tile([P, PASSES * B], U8, align_bytes=64)
         head_codes = operands.tile([P, 2 * LOAD_CODES], U32, align_bytes=64)
         head_scales = operands.tile([P, 2 * LOAD_CODES], U8, align_bytes=64)
         h2_codes = operands.tile([P, PASSES * B], U32, align_bytes=64)
@@ -133,31 +134,38 @@ def tile_rdecommunicationlstm_pb_kernel(
         h1_rows = h1.rearrange("(p j) k -> p j k", j=B_TILES)
         w_rows = W_ih1.rearrange("(q g p t) k -> g t p q k", q=GATES, g=PASSES, p=P, t=PACK)
 
-        def source(rows, planes, block, codes, scales, index):
-            cols = slice(index * LOAD_CODES, (index + 1) * LOAD_CODES)
-            return {"rows": rows, "planes": planes, "block": block, "codes": codes[:, cols], "scales": scales[:, cols]}
+        def source(rows, tiles, planes, block, codes, scales, start):
+            cols = slice(start, start + tiles * PASSES * P)
+            return {
+                "rows": rows, "tiles": tiles, "planes": planes, "block": block,
+                "codes": codes[:, cols], "scales": scales[:, cols],
+            }
 
-        def h1_source(half):
-            rows = h1_rows[:, half * HALF_TILES : (half + 1) * HALF_TILES, :]
-            return source(rows, split_planes, moving_block, h1_codes, h1_scales, half)
+        def h1_source(part):
+            tiles, first = PARTS[part], PART_START[part]
+            rows = h1_rows[:, first : first + tiles, :]
+            return source(rows, tiles, split_planes, moving_block, h1_codes, h1_scales, first * PASSES * P)
+
+        def w_source(s):
+            rows = w_rows[s // PACK, s % PACK]
+            return source(rows, GATES, split_planes, stationary_block, w_codes, w_scales, s * LOAD_CODES)
 
         def head_source(weights, head):
             rows = weights.rearrange("(j p) k -> p j k", p=P)
-            return source(rows, alternate_planes, moving_block, head_codes, head_scales, head)
+            return source(rows, ROW_TILES, alternate_planes, moving_block, head_codes, head_scales, head * LOAD_CODES)
 
-        sources = [h1_source(0)]
-        for s in range(SLICES):
-            sources.append(source(w_rows[s // PACK, s % PACK], split_planes, stationary_block, w_codes, w_scales, s))
+        sources = [h1_source(0)] + [w_source(s) for s in range(SLICES)]
         sources.extend([h1_source(1), head_source(mu_W, 0), head_source(sig_W, 1)])
         raw_words = {}
         banks = {}
         grouped = {}
 
-        def load_rows(r):
+        def load_rows(r, step=2):
+            tiles = sources[r]["tiles"]
             raw = raw_pool.tile([P, ROW_TILES * HID], BF16, tag="raw")
             row_tiles = raw[:].rearrange("p (a k) -> p a k", a=ROW_TILES)
-            for pair in (slice(0, ROW_TILES // 2), slice(ROW_TILES // 2, ROW_TILES)):
-                nc.sync.dma_start(out=row_tiles[:, pair, :], in_=sources[r]["rows"][:, pair, :])
+            for a in range(0, tiles, step):
+                nc.sync.dma_start(out=row_tiles[:, a : a + step, :], in_=sources[r]["rows"][:, a : a + step, :])
             raw_words[r] = raw[:].bitcast(F32).rearrange("p (a w) -> p a w", a=ROW_TILES)
             if r == len(sources) - 1:
                 for v, vec in enumerate((mu_b, ln_g, ln_b, sig_b)):
@@ -168,28 +176,31 @@ def tile_rdecommunicationlstm_pb_kernel(
                 idle = psum_gates.tile([P, BANK], F32, tag="gate")
                 nc.tensor.matmul(out=idle[:], lhsT=zeros[:, :P], rhs=zeros[:], start=True, stop=True)
 
+        def transpose_bank(r, b):
+            bank = psum_aux.tile([P, 2, 2, P], F32, tag="aux")
+            for d in range(2):
+                a, c = sources[r]["block"](sources[r]["tiles"], b, d)
+                for u, plane in enumerate(sources[r]["planes"](raw_words[r], a, c)):
+                    nc.tensor.transpose(out=bank[:, d, u, :], in_=plane, identity=ident[:])
+            banks[(r, b)] = bank
+            if b == 0:
+                group_tile = stage.tile([P, LOAD_CODES * PACK], BF16, tag="grouped", align_bytes=64)
+                grouped[r] = group_tile
+
         def transpose_rows(r):
-            for b in range(BANKS):
-                bank = psum_aux.tile([P, 2, 2, P], F32, tag="aux")
-                for d in range(2):
-                    a, c = sources[r]["block"](b, d)
-                    for u, plane in enumerate(sources[r]["planes"](raw_words[r], a, c)):
-                        nc.tensor.transpose(out=bank[:, d, u, :], in_=plane, identity=ident[:])
-                banks[(r, b)] = bank
-            group_tile = stage.tile([P, LOAD_CODES * PACK], BF16, tag="grouped", align_bytes=64)
-            grouped[r] = group_tile
+            for b in range(sources[r]["tiles"]):
+                transpose_bank(r, b)
 
         def empty_bank(r, b, copy):
             words = grouped[r][:].bitcast(F32).rearrange("p (b d row u) -> p b d row u", b=BANKS, d=2, row=P, u=2)
             copy(out=words[:, b], in_=banks[(r, b)][:].rearrange("p d u row -> p d row u"))
 
-        def quantise_half(r, h):
-            half_codes = LOAD_CODES // 2
-            cols = slice(h * half_codes, (h + 1) * half_codes)
+        def quantise_banks(r, first, count):
+            cols = slice(first * 2 * P, (first + count) * 2 * P)
             nc.vector.quantize_mx(
                 out=sources[r]["codes"][:, cols].bitcast(FP8X4),
                 scales=sources[r]["scales"][:, cols],
-                in_=grouped[r][:, h * half_codes * PACK : (h + 1) * half_codes * PACK],
+                in_=grouped[r][:, first * 2 * P * PACK : (first + count) * 2 * P * PACK],
             )
 
         gate_acc = {}
@@ -199,18 +210,21 @@ def tile_rdecommunicationlstm_pb_kernel(
         groups = {}
         hidden = {}
 
+        def width(n):
+            return PARTS[n // SLICES] * P
+
         def gate_product(n, q):
-            half, s = divmod(n, SLICES)
+            part, s = divmod(n, SLICES)
             acc = psum_gates.tile([P, BANK], F32, tag="gate")
             for c in range(PASSES):
                 w_start = ((s * GATES + q) * PASSES + c) * P
-                x_start = (half * PASSES + c) * BANK
+                x_start = PASSES * P * PART_START[part] + c * width(n)
                 nc.tensor.matmul_mx(
-                    out=acc[:],
+                    out=acc[:, : width(n)],
                     lhsT=w_codes[:, w_start : w_start + P].bitcast(FP8X4),
                     lhsT_scale=w_scales[:, w_start : w_start + P],
-                    rhs=h1_codes[:, x_start : x_start + BANK].bitcast(FP8X4),
-                    rhs_scale=h1_scales[:, x_start : x_start + BANK],
+                    rhs=h1_codes[:, x_start : x_start + width(n)].bitcast(FP8X4),
+                    rhs_scale=h1_scales[:, x_start : x_start + width(n)],
                     start=(c == 0),
                     stop=(c == PASSES - 1),
                 )
@@ -224,14 +238,14 @@ def tile_rdecommunicationlstm_pb_kernel(
                     o_group = group_pool.tile([P, PACK, BANK], F32, tag="o", bufs=3)
                     tanh_group = group_pool.tile([P, PACK, BANK], F32, tag="tanh_c")
                     groups[n // PACK] = (o_group, tanh_group)
-                value = groups[n // PACK][0][:, t, :]
+                value = groups[n // PACK][0][:, t, : width(n)]
             else:
                 gate_tile = gate_pool.tile([P, BANK], F32, tag="gate%d" % q)
-                value = gate_tile[:]
+                value = gate_tile[:, : width(n)]
             col = (q * PASSES + s // PACK) * PACK + t
             nc.scalar.activation(
                 out=value,
-                in_=gate_acc[(n, q)][:],
+                in_=gate_acc[(n, q)][:, : width(n)],
                 func=ACT.Tanh if q == GATE_G else ACT.Sigmoid,
                 bias=gate_bias[:, col : col + 1],
                 scale=1.0,
@@ -244,21 +258,20 @@ def tile_rdecommunicationlstm_pb_kernel(
                 gate_product(n + 1, q)
 
         def cell_input(n):
-            input_term = gate_pool.tile([P, BANK], F32, tag="input_term")
-            nc.vector.tensor_tensor(out=input_term[:], in0=gate_out[(n, GATE_I)], in1=gate_out[(n, GATE_G)], op=ALU.mult)
-            input_terms[n] = input_term
+            term = gate_pool.tile([P, BANK], F32, tag="input_term")
+            input_terms[n] = term[:, : width(n)]
+            nc.vector.tensor_tensor(out=input_terms[n], in0=gate_out[(n, GATE_I)], in1=gate_out[(n, GATE_G)], op=ALU.mult)
 
         def cell_new(n):
             s = n % SLICES
-            cell = gate_pool.tile([P, BANK], F32, tag="cell")
+            cells[n] = input_terms[n]
             nc.vector.scalar_tensor_tensor(
-                out=cell[:], in0=gate_out[(n, GATE_F)], scalar=cell0[:, s : s + 1], in1=input_terms[n][:],
+                out=cells[n], in0=gate_out[(n, GATE_F)], scalar=cell0[:, s : s + 1], in1=input_terms[n],
                 op0=ALU.mult, op1=ALU.add,
             )
-            cells[n] = cell
 
         def cell_tanh(n):
-            nc.scalar.activation(out=groups[n // PACK][1][:, n % PACK, :], in_=cells[n][:], func=ACT.Tanh)
+            nc.scalar.activation(out=groups[n // PACK][1][:, n % PACK, : width(n)], in_=cells[n], func=ACT.Tanh)
 
         def hidden_product(grp, jj):
             o_group, tanh_group = groups[grp]
@@ -273,8 +286,8 @@ def tile_rdecommunicationlstm_pb_kernel(
             hidden[(grp, jj)] = h2_grouped
 
         def hidden_quantise(grp, jj):
-            half, g = divmod(grp, PASSES)
-            start = g * B + (half * HALF_TILES + jj) * P
+            part, g = divmod(grp, PASSES)
+            start = g * B + (PART_START[part] + jj) * P
             nc.vector.quantize_mx(
                 out=h2_codes[:, start : start + P].bitcast(FP8X4),
                 scales=h2_scales[:, start : start + P],
@@ -288,8 +301,8 @@ def tile_rdecommunicationlstm_pb_kernel(
         head_acc = {}
         mean_tiles = {}
 
-        def head_product(j, head):
-            acc = psum_aux.tile([P, BANK], F32, tag="aux")
+        def head_product(j, head, pool=psum_aux, tag="aux"):
+            acc = pool.tile([P, BANK], F32, tag=tag)
             for c in range(PASSES):
                 b_start = c * B + j * P
                 col_start = (head * PASSES + c) * OUT
@@ -305,7 +318,7 @@ def tile_rdecommunicationlstm_pb_kernel(
             head_acc[(j, head)] = acc
 
         def mean_sum(j):
-            mu_lin = head_pool.tile([P, OUT], F32, tag="mu_lin")
+            mu_lin = head_pool.tile([P, OUT], F32, tag="mu_lin", bufs=4)
             row_sum = small.tile([P, 1], F32, tag="row_sum")
             nc.vector.scalar_tensor_tensor(
                 out=mu_lin[:], in0=head_acc[(j, 0)][:], scalar=1.0, in1=mu_b_rows, op0=ALU.mult, op1=ALU.add,
@@ -366,78 +379,89 @@ def tile_rdecommunicationlstm_pb_kernel(
             )
             nc.sync.dma_start(out=sigma_out[:, j, :], in_=spread_in[:, j, :])
 
-        def piece(m):
-            return m // HALF_TILES, m % HALF_TILES
-
+        VECTOR, SCALAR = nc.vector.tensor_copy, nc.scalar.copy
         load_rows(0)
         load_vectors()
         for r in range(1, RAW_BUFS):
             load_rows(r)
-        keep_warm(WARM_START)
-        for r in range(2):
-            transpose_rows(r)
-            load_rows(r + RAW_BUFS)
-            for b in range(BANKS):
-                empty_bank(r, b, nc.scalar.copy)
-            for h in range(2):
-                quantise_half(r, h)
-            if r == 0:
-                turn_vectors()
-        gate_product(0, GATE_I)
-        gate_product(0, GATE_F)
-        transpose_rows(2)
-        gate_product(0, GATE_G)
-        gate_product(0, GATE_O)
-        load_rows(2 + RAW_BUFS)
+        keep_warm(6)
+        transpose_rows(0)
+        load_rows(RAW_BUFS)
         for b in range(BANKS):
-            empty_bank(2, b, nc.vector.tensor_copy)
-        for h in range(2):
-            quantise_half(2, h)
+            empty_bank(0, b, SCALAR)
+        quantise_banks(0, 0, 2)
+        quantise_banks(0, 2, 2)
+        turn_vectors()
+        transpose_rows(1)
+        load_rows(1 + RAW_BUFS)
+        for b in range(BANKS):
+            empty_bank(1, b, SCALAR)
+        quantise_banks(1, 0, 2)
+        transpose_bank(2, 0)
+        transpose_bank(2, 1)
+        empty_bank(2, 0, VECTOR)
+        quantise_banks(1, 2, 2)
+        empty_bank(2, 1, VECTOR)
+        gate_product(0, 0)
+        gate_product(0, 1)
+        transpose_bank(2, 2)
+        transpose_bank(2, 3)
+        gate_product(0, 2)
+        gate_product(0, 3)
+        load_rows(2 + RAW_BUFS)
+        empty_bank(2, 2, VECTOR)
+        quantise_banks(2, 0, 2)
+        empty_bank(2, 3, VECTOR)
+        quantise_banks(2, 2, 2)
         transpose_rows(3)
         load_rows(3 + RAW_BUFS)
 
+        def piece(m):
+            return m // PARTS[0], m % PARTS[0]
+
         HIDDEN_LAG = PACK + 1
-        FIRST_HEAD = HALF_TILES + HIDDEN_LAG + 1
+        FIRST_HEAD = PARTS[0] + HIDDEN_LAG + 1
+        HEADS0 = PARTS[0]
         for n in range(UNITS):
             r = n + 3
             m = n - HIDDEN_LAG
             j = n - FIRST_HEAD
             loading = r < len(sources)
-            heads = 0 <= j < HALF_TILES
+            heads = 0 <= j < HEADS0
             if heads:
                 head_product(j, 0)
                 head_product(j, 1)
             if n > 0:
                 cell_input(n - 1)
             if 3 < r <= len(sources):
-                quantise_half(r - 1, 1)
+                quantise_banks(r - 1, 2, 2)
             if m >= 0:
                 hidden_product(*piece(m))
             if loading:
-                empty_bank(r, 0, nc.vector.tensor_copy)
+                empty_bank(r, 0, VECTOR)
             if loading:
-                empty_bank(r, 1, nc.vector.tensor_copy)
-            if heads:
-                mean_sum(j)
+                empty_bank(r, 1, VECTOR)
             if n > 0:
                 cell_new(n - 1)
+            if heads:
+                mean_sum(j)
             if m >= 0:
                 hidden_quantise(*piece(m))
+            if 0 <= j - 1 < HEADS0:
+                mean_finish(j - 1)
             if heads:
                 mean_centre(j)
             if loading:
-                quantise_half(r, 0)
+                quantise_banks(r, 0, 2)
             if heads:
                 spread_sum(j)
             if heads:
                 mean_scale(j)
-            if 0 <= j - 1 < HALF_TILES:
-                mean_finish(j - 1)
             for q in range(GATES):
                 gate(n, q)
             if loading:
-                empty_bank(r, 2, nc.scalar.copy)
-                empty_bank(r, 3, nc.scalar.copy)
+                empty_bank(r, 2, SCALAR)
+                empty_bank(r, 3, SCALAR)
             if n > 0:
                 cell_tanh(n - 1)
             if heads:
@@ -447,29 +471,40 @@ def tile_rdecommunicationlstm_pb_kernel(
                 if r + 1 + RAW_BUFS < len(sources):
                     load_rows(r + 1 + RAW_BUFS)
 
-        cell_input(UNITS - 1)
-        cell_new(UNITS - 1)
-        cell_tanh(UNITS - 1)
-        spread_sigmoid(slice(0, HALF_TILES))
         first_left = UNITS - HIDDEN_LAG
+        cell_input(UNITS - 1)
         hidden_product(*piece(first_left))
-        for m in range(first_left + 1, PIECES):
+        cell_new(UNITS - 1)
+        hidden_quantise(*piece(first_left))
+        cell_tanh(UNITS - 1)
+        spread_sigmoid(slice(0, HEADS0))
+        for m in range(first_left + 1, 16):
             hidden_product(*piece(m))
-            hidden_quantise(*piece(m - 1))
-        hidden_quantise(*piece(PIECES - 1))
-        for j in range(HALF_TILES, B_TILES + 2):
-            if j < B_TILES:
-                head_product(j, 0)
-                head_product(j, 1)
+            if m > first_left + 1:
+                hidden_quantise(*piece(m - 1))
+        late = range(HEADS0, B_TILES)
+        for j in late:
+            head_product(j, 0)
+            if j == HEADS0:
                 mean_sum(j)
-                spread_sum(j)
-                mean_centre(j)
-                mean_deviation(j)
-                spread_sigmoid(j)
-            if HALF_TILES <= j - 1 < B_TILES:
-                mean_scale(j - 1)
-            if HALF_TILES <= j - 2:
-                mean_finish(j - 2)
-        for j in range(B_TILES):
+                hidden_quantise(*piece(15))
+            else:
+                mean_sum(j)
+            head_product(j, 1, *((psum_gates, "gate") if j >= 6 else ()))
+            spread_sum(j)
+            mean_centre(j)
+            mean_deviation(j)
+            spread_sigmoid(j)
+        mean_scale(4)
+        mean_scale(5)
+        mean_finish(4)
+        mean_scale(6)
+        mean_finish(5)
+        mean_scale(7)
+        mean_finish(6)
+        spread_ln(0)
+        spread_finish(0)
+        mean_finish(7)
+        for j in range(1, B_TILES):
             spread_ln(j)
             spread_finish(j)

@@ -328,7 +328,9 @@ def tile_rdecommunicationlstm_pb_kernel(
 
         def mean_centre(j):
             neg_mean = small.tile([P, 1], F32, tag="neg_mean")
-            nc.vector.tensor_scalar_mul(out=neg_mean[:], in0=mean_tiles[j]["row_sum"][:], scalar1=-1.0 / OUT)
+            nc.gpsimd.tensor_scalar(
+                out=neg_mean[:], in0=mean_tiles[j]["row_sum"][:], scalar1=-1.0 / OUT, scalar2=0.0, op0=ALU.mult, op1=ALU.add
+            )
             mean_tiles[j]["neg_mean"] = neg_mean
 
         def mean_scale(j):
@@ -343,12 +345,12 @@ def tile_rdecommunicationlstm_pb_kernel(
             squares = head_pool.tile([P, OUT], F32, tag="squares", bufs=1)
             square_sum = small.tile([P, 1], F32, tag="square_sum")
             nc.scalar.activation(
-                out=squares[:], in_=mean_tiles[j]["mu_lin"][:], func=ACT.Square, bias=mean_tiles[j]["neg_mean"][:],
-                scale=1.0, accum_out=square_sum[:],
+                out=squares[:], in_=mean_tiles[j]["mu_lin"][:], func=ACT.Square, bias=mean_tiles[j]["row_sum"][:],
+                scale=-1.0 * OUT, accum_out=square_sum[:],
             )
             var_eps = small.tile([P, 1], F32, tag="var_eps")
             nc.gpsimd.tensor_scalar(
-                out=var_eps[:], in0=square_sum[:], scalar1=1.0 / OUT, scalar2=LN_EPS, op0=ALU.mult, op1=ALU.add
+                out=var_eps[:], in0=square_sum[:], scalar1=1.0 / OUT**3, scalar2=LN_EPS, op0=ALU.mult, op1=ALU.add
             )
             rstd = small.tile([P, 1], F32, tag="rstd")
             nc.gpsimd.tensor_tensor(out=rstd[:], in0=var_eps[:], in1=neg_half[:], op=ALU.pow)

@@ -171,10 +171,10 @@ def tile_rdecommunicationlstm_pb_kernel(
                 for v, vec in enumerate((mu_b, ln_g, ln_b, sig_b)):
                     nc.sync.dma_start(out=row_vectors[:, v, :], in_=vec.partition_broadcast(P))
 
-        def keep_warm(count):
+        def keep_warm(count, moving=zeros):
             for turn in range(count):
                 idle = psum_gates.tile([P, BANK], F32, tag="gate")
-                nc.tensor.matmul(out=idle[:], lhsT=zeros[:, :P], rhs=zeros[:], start=True, stop=True)
+                nc.tensor.matmul(out=idle[:], lhsT=zeros[:, :P], rhs=moving[:], start=True, stop=True)
 
         def transpose_bank(r, b):
             bank = psum_aux.tile([P, 2, 2, P], F32, tag="aux")
@@ -388,13 +388,17 @@ def tile_rdecommunicationlstm_pb_kernel(
             load_rows(r)
         keep_warm(6)
         transpose_rows(0)
+        keep_warm(2)
         load_rows(RAW_BUFS)
         for b in range(BANKS):
             empty_bank(0, b, SCALAR)
         quantise_banks(0, 0, 2)
         quantise_banks(0, 2, 2)
         turn_vectors()
-        transpose_rows(1)
+        transpose_bank(1, 0)
+        transpose_bank(1, 1)
+        transpose_bank(1, 2)
+        transpose_bank(1, 3)
         load_rows(1 + RAW_BUFS)
         for b in range(BANKS):
             empty_bank(1, b, SCALAR)
@@ -443,10 +447,10 @@ def tile_rdecommunicationlstm_pb_kernel(
                 empty_bank(r, 0, VECTOR)
             if loading:
                 empty_bank(r, 1, VECTOR)
-            if n > 0:
-                cell_new(n - 1)
             if heads:
                 mean_sum(j)
+            if n > 0:
+                cell_new(n - 1)
             if m >= 0:
                 hidden_quantise(*piece(m))
             if 0 <= j - 1 < HEADS0:
@@ -475,13 +479,17 @@ def tile_rdecommunicationlstm_pb_kernel(
 
         first_left = UNITS - HIDDEN_LAG
         cell_input(UNITS - 1)
+        keep_warm(0)
         hidden_product(*piece(first_left))
+        keep_warm(2, hidden[piece(first_left)])
         cell_new(UNITS - 1)
         hidden_quantise(*piece(first_left))
         cell_tanh(UNITS - 1)
         spread_sigmoid(slice(0, HEADS0))
         for m in range(first_left + 1, 16):
             hidden_product(*piece(m))
+            if m == first_left + 1:
+                keep_warm(0, hidden[piece(m)])
             if m > first_left + 1:
                 hidden_quantise(*piece(m - 1))
         late = range(HEADS0, B_TILES)

import math
from contextlib import ExitStack

import concourse.mybir as mybir
from concourse.masks import make_identity

FP8X4 = mybir.dt.float8_e4m3fn_x4
BF16 = mybir.dt.bfloat16
F32 = mybir.dt.float32
U32 = mybir.dt.uint32
U8 = mybir.dt.uint8
ACT = mybir.ActivationFunctionType
ALU = mybir.AluOpType

P = 128
PACK = 4
K_PASS = P * PACK
BANK = 512

B, HID, OUT, GATES = 1024, 1024, 512, 4
PASSES = HID // K_PASS
ROW_TILES = 4
PASS_WORDS = K_PASS // 2
LOAD_CODES = ROW_TILES * PASSES * P
BANKS = ROW_TILES * PASSES // 2
B_TILES = B // P
SLICES = HID // P
PARTS = (4, 4)
PART_START = [sum(PARTS[:part]) for part in range(len(PARTS))]
UNITS = len(PARTS) * SLICES
GATE_I, GATE_F, GATE_G, GATE_O = 0, 1, 2, 3
LN_EPS = 1e-5
SIG_MIN = 1e-6
TINY = 2.0**-100
WARM_START = 6
RAW_BUFS = 4
RUN = 4

FLOPS = 2 * B * HID * (GATES * HID + 2 * OUT)


def split_planes(words, a, c):
    start = c * PASS_WORDS
    return [words[:, a, start + u * P : start + (u + 1) * P] for u in range(2)]


def alternate_planes(words, a, c):
    start = c * PASS_WORDS
    return [words[:, a, start + u : start + PASS_WORDS : 2] for u in range(2)]


def stationary_block(tiles, bank, d):
    return bank, d


def moving_block(tiles, bank, d):
    c, a = divmod(2 * bank + d, tiles)
    return a, c


def tile_rdecommunicationlstm_pb_kernel(
    tc, h1, W_ih1, hh_gates, b_ih1, b_hh1, c_init, mu_W, mu_b, ln_g, ln_b, sig_W, sig_b, out_0, out_1
):
    nc = tc.nc
    with ExitStack() as ctx:
        ctx.enter_context(tc.manual_schedule())
        consts = ctx.enter_context(tc.tile_pool(name="consts", bufs=1))
        operands = ctx.enter_context(tc.tile_pool(name="operands", bufs=1))
        raw_pool = ctx.enter_context(tc.tile_pool(name="raw", bufs=RAW_BUFS))
        stage = ctx.enter_context(tc.tile_pool(name="stage", bufs=2))
        gate_pool = ctx.enter_context(tc.tile_pool(name="gates", bufs=2))
        group_pool = ctx.enter_context(tc.tile_pool(name="groups", bufs=2))
        head_pool = ctx.enter_context(tc.tile_pool(name="heads", bufs=3))
        small = ctx.enter_context(tc.tile_pool(name="small", bufs=4))
        psum_gates = ctx.enter_context(tc.psum_pool(name="psum_gates", bufs=GATES))
        psum_aux = ctx.enter_context(tc.psum_pool(name="psum_aux", bufs=BANKS))

        ident = consts.tile([P, P], F32)
        make_identity(nc, ident[:])
        zeros = consts.tile([P, BANK], BF16)
        nc.vector.memset(zeros[:], 0.0)
        neg_half = consts.tile([P, 1], F32)
        nc.vector.memset(neg_half[:], -0.5)
        tiny = consts.tile([P, 1], F32)
        nc.vector.memset(tiny[:], TINY)
        warm = consts.tile([P, 1], F32)
        nc.vector.memset(warm[:], 0.0)
        nc.scalar.activation(out=warm[:], in_=warm[:], func=ACT.Sigmoid)

        VECTOR_BLOCKS = GATES * PASSES
        VECTOR_ROWS = 3 * VECTOR_BLOCKS + PASSES
        BIAS_COLS = VECTOR_BLOCKS * PACK
        vector_rows = consts.tile([P, K_PASS], BF16)
        nc.vector.memset(vector_rows[:], 0.0)
        vector_cols = consts.tile([P, VECTOR_ROWS * PACK], BF16)
        gate_bias = consts.tile([P, BIAS_COLS], F32)
        cell0 = consts.tile([P, SLICES], F32)

        def load_vectors():
            for v, vec in enumerate((hh_gates, b_ih1, b_hh1)):
                nc.sync.dma_start(
                    out=vector_rows[v * VECTOR_BLOCKS : (v + 1) * VECTOR_BLOCKS, :],
                    in_=vec.rearrange("(blk i) -> blk i", i=K_PASS),
                )
            nc.sync.dma_start(
                out=vector_rows[3 * VECTOR_BLOCKS : VECTOR_ROWS, :], in_=c_init.rearrange("(blk i) -> blk i", i=K_PASS)
            )

        def turn_vectors():
            vector_bank = psum_aux.tile([P, 2, P], F32, tag="aux")
            for u in range(2):
                nc.tensor.transpose(out=vector_bank[:, u, :], in_=vector_rows[:].bitcast(F32)[:, u::2], identity=ident[:])
            nc.vector.tensor_copy(
                out=vector_cols[:].bitcast(F32).rearrange("p (row u) -> p row u", u=2),
                in_=vector_bank[:, :, :VECTOR_ROWS].rearrange("p u row -> p row u"),
            )
            hh_cols, ih_cols, bhh_cols = [vector_cols[:, v * BIAS_COLS : (v + 1) * BIAS_COLS] for v in range(3)]
            nc.vector.tensor_tensor(out=gate_bias[:], in0=ih_cols, in1=bhh_cols, op=ALU.add)
            nc.vector.tensor_copy(out=cell0[:], in_=vector_cols[:, 3 * BIAS_COLS :])
            nc.vector.tensor_tensor(out=gate_bias[:], in0=gate_bias[:], in1=hh_cols, op=ALU.add)

        row_vectors = consts.tile([P, 4, OUT], BF16)
        mu_b_rows, ln_g_rows, ln_b_rows, sig_b_rows = [row_vectors[:, v, :] for v in range(4)]

        w_codes = operands.tile([P, SLICES * LOAD_CODES], U32, align_bytes=64)
        w_scales = operands.tile([P, SLICES * LOAD_CODES], U8, align_bytes=64)
        h1_codes = operands.tile([P, PASSES * B], U32, align_bytes=64)
        h1_scales = operands.tile([P, PASSES * B], U8, align_bytes=64)
        head_codes = operands.tile([P, 2 * LOAD_CODES], U32, align_bytes=64)
        head_scales = operands.tile([P, 2 * LOAD_CODES], U8, align_bytes=64)
        h2_codes = operands.tile([P, PASSES * B], U32, align_bytes=64)
        h2_scales = operands.tile([P, PASSES * B], U8, align_bytes=64)

        h1_rows = h1.rearrange("(p j) k -> p j k", j=B_TILES)
        w_rows = W_ih1.rearrange("(q g p t) k -> g t p q k", q=GATES, g=PASSES, p=P, t=PACK)

        def source(rows, tiles, planes, block, codes, scales, start):
            cols = slice(start, start + tiles * PASSES * P)
            return {
                "rows": rows, "tiles": tiles, "planes": planes, "block": block,
                "codes": codes[:, cols], "scales": scales[:, cols],
            }

        def h1_source(part):
            tiles, first = PARTS[part], PART_START[part]
            rows = h1_rows[:, first : first + tiles, :]
            return source(rows, tiles, split_planes, moving_block, h1_codes, h1_scales, first * PASSES * P)

        def w_source(s):
            rows = w_rows[s // PACK, s % PACK]
            return source(rows, GATES, split_planes, stationary_block, w_codes, w_scales, s * LOAD_CODES)

        def head_source(weights, head):
            rows = weights.rearrange("(j p) k -> p j k", p=P)
            return source(rows, ROW_TILES, alternate_planes, moving_block, head_codes, head_scales, head * LOAD_CODES)

        sources = [h1_source(0)] + [w_source(s) for s in range(SLICES)]
        sources.extend([h1_source(1), head_source(mu_W, 0), head_source(sig_W, 1)])
        raw_words = {}
        banks = {}
        grouped = {}

        def load_rows(r, step=2):
            tiles = sources[r]["tiles"]
            raw = raw_pool.tile([P, ROW_TILES * HID], BF16, tag="raw")
            row_tiles = raw[:].rearrange("p (a k) -> p a k", a=ROW_TILES)
            for a in range(0, tiles, step):
                nc.sync.dma_start(out=row_tiles[:, a : a + step, :], in_=sources[r]["rows"][:, a : a + step, :])
            raw_words[r] = raw[:].bitcast(F32).rearrange("p (a w) -> p a w", a=ROW_TILES)
            if r == len(sources) - 1:
                for v, vec in enumerate((mu_b, ln_g, ln_b, sig_b)):
                    nc.sync.dma_start(out=row_vectors[:, v, :], in_=vec.partition_broadcast(P))

        def keep_warm(count, moving=zeros):
            for turn in range(count):
                idle = psum_gates.tile([P, BANK], F32, tag="gate")
                nc.tensor.matmul(out=idle[:], lhsT=zeros[:, :P], rhs=moving[:], start=True, stop=True)

        def transpose_bank(r, b):
            bank = psum_aux.tile([P, 2, 2, P], F32, tag="aux")
            for d in range(2):
                a, c = sources[r]["block"](sources[r]["tiles"], b, d)
                for u, plane in enumerate(sources[r]["planes"](raw_words[r], a, c)):
                    nc.tensor.transpose(out=bank[:, d, u, :], in_=plane, identity=ident[:])
            banks[(r, b)] = bank
            if b == 0:
                group_tile = stage.tile([P, LOAD_CODES * PACK], BF16, tag="grouped", align_bytes=64)
                grouped[r] = group_tile

        def transpose_rows(r):
            for b in range(sources[r]["tiles"]):
                transpose_bank(r, b)

        def empty_bank(r, b, copy):
            words = grouped[r][:].bitcast(F32).rearrange("p (b d row u) -> p b d row u", b=BANKS, d=2, row=P, u=2)
            copy(out=words[:, b], in_=banks[(r, b)][:].rearrange("p d u row -> p d row u"))

        def quantise_banks(r, first, count):
            cols = slice(first * 2 * P, (first + count) * 2 * P)
            nc.vector.quantize_mx(
                out=sources[r]["codes"][:, cols].bitcast(FP8X4),
                scales=sources[r]["scales"][:, cols],
                in_=grouped[r][:, first * 2 * P * PACK : (first + count) * 2 * P * PACK],
            )

        gate_acc = {}
        gate_out = {}
        input_terms = {}
        cells = {}
        groups = {}
        hidden = {}

        def width(n):
            return PARTS[n // SLICES] * P

        def gate_product(n, q):
            part, s = divmod(n, SLICES)
            acc = psum_gates.tile([P, BANK], F32, tag="gate")
            for c in range(PASSES):
                w_start = ((s * GATES + q) * PASSES + c) * P
                x_start = PASSES * P * PART_START[part] + c * width(n)
                nc.tensor.matmul_mx(
                    out=acc[:, : width(n)],
                    lhsT=w_codes[:, w_start : w_start + P].bitcast(FP8X4),
                    lhsT_scale=w_scales[:, w_start : w_start + P],
                    rhs=h1_codes[:, x_start : x_start + width(n)].bitcast(FP8X4),
                    rhs_scale=h1_scales[:, x_start : x_start + width(n)],
                    start=(c == 0),
                    stop=(c == PASSES - 1),
                )
            gate_acc[(n, q)] = acc

        def gate_function(n, q):
            s = n % SLICES
            t = s % PACK
            if q == GATE_O:
                if t == 0:
                    o_group = group_pool.tile([P, PACK, BANK], F32, tag="o", bufs=3)
                    tanh_group = group_pool.tile([P, PACK, BANK], F32, tag="tanh_c")
                    groups[n // PACK] = (o_group, tanh_group)
                value = groups[n // PACK][0][:, t, : width(n)]
            else:
                gate_tile = gate_pool.tile([P, BANK], F32, tag="gate%d" % q)
                value = gate_tile[:, : width(n)]
            col = (q * PASSES + s // PACK) * PACK + t
            nc.scalar.activation(
                out=value,
                in_=gate_acc[(n, q)][:, : width(n)],
                func=ACT.Tanh if q == GATE_G else ACT.Sigmoid,
                bias=gate_bias[:, col : col + 1],
                scale=1.0,
            )
            gate_out[(n, q)] = value

        def gate(n, q):
            gate_function(n, q)
            if n + 1 < UNITS:
                gate_product(n + 1, q)

        def cell_input(n):
            term = gate_pool.tile([P, BANK], F32, tag="input_term")
            input_terms[n] = term[:, : width(n)]
            nc.vector.tensor_tensor(out=input_terms[n], in0=gate_out[(n, GATE_I)], in1=gate_out[(n, GATE_G)], op=ALU.mult)

        def cell_new(n):
            s = n % SLICES
            cells[n] = input_terms[n]
            nc.vector.scalar_tensor_tensor(
                out=cells[n], in0=gate_out[(n, GATE_F)], scalar=cell0[:, s : s + 1], in1=input_terms[n],
                op0=ALU.mult, op1=ALU.add,
            )

        def cell_tanh(n):
            nc.scalar.activation(out=groups[n // PACK][1][:, n % PACK, : width(n)], in_=cells[n], func=ACT.Tanh)

        def hidden_product(grp, jj):
            o_group, tanh_group = groups[grp]
            batch_rows = slice(jj * P, (jj + 1) * P)
            h2_grouped = stage.tile([P, P * PACK], BF16, tag="h2", align_bytes=64, bufs=3)
            nc.vector.tensor_tensor(
                out=h2_grouped[:].rearrange("p (run i t) -> p run t i", i=RUN, t=PACK),
                in0=o_group[:, :, batch_rows].rearrange("p t (run i) -> p run t i", i=RUN),
                in1=tanh_group[:, :, batch_rows].rearrange("p t (run i) -> p run t i", i=RUN),
                op=ALU.mult,
            )
            hidden[(grp, jj)] = h2_grouped

        def hidden_quantise(grp, jj):
            part, g = divmod(grp, PASSES)
            start = g * B + (PART_START[part] + jj) * P
            nc.vector.quantize_mx(
                out=h2_codes[:, start : start + P].bitcast(FP8X4),
                scales=h2_scales[:, start : start + P],
                in_=hidden[(grp, jj)][:],
            )

        mu_out = out_0.rearrange("(p j) col -> p j col", j=B_TILES)
        sigma_out = out_1.rearrange("(p j) col -> p j col", j=B_TILES)
        spread_in = head_pool.tile([P, B_TILES, OUT], F32, tag="spread_in", bufs=1)
        spread_log = head_pool.tile([P, B_TILES, OUT], F32, tag="spread_log", bufs=1)
        head_acc = {}
        mean_tiles = {}

        def head_product(j, head, pool=psum_aux, tag="aux"):
            acc = pool.tile([P, BANK], F32, tag=tag)
            for c in range(PASSES):
                b_start = c * B + j * P
                col_start = (head * PASSES + c) * OUT
                nc.tensor.matmul_mx(
                    out=acc[:],
                    lhsT=h2_codes[:, b_start : b_start + P].bitcast(FP8X4),
                    lhsT_scale=h2_scales[:, b_start : b_start + P],
                    rhs=head_codes[:, col_start : col_start + OUT].bitcast(FP8X4),
                    rhs_scale=head_scales[:, col_start : col_start + OUT],
                    start=(c == 0),
                    stop=(c == PASSES - 1),
                )
            head_acc[(j, head)] = acc

        def mean_sum(j):
            mu_lin = head_pool.tile([P, OUT], F32, tag="mu_lin", bufs=4)
            row_sum = small.tile([P, 1], F32, tag="row_sum")
            nc.vector.scalar_tensor_tensor(
                out=mu_lin[:], in0=head_acc[(j, 0)][:], scalar=1.0, in1=mu_b_rows, op0=ALU.mult, op1=ALU.add,
                accum_out=row_sum[:],
            )
            mean_tiles[j] = {"mu_lin": mu_lin, "row_sum": row_sum}

        def mean_centre(j):
            neg_mean = small.tile([P, 1], F32, tag="neg_mean")
            nc.gpsimd.tensor_scalar(
                out=neg_mean[:], in0=mean_tiles[j]["row_sum"][:], scalar1=-1.0 / OUT, scalar2=0.0, op0=ALU.mult, op1=ALU.add
            )
            mean_tiles[j]["neg_mean"] = neg_mean

        def mean_scale(j):
            scaled = head_pool.tile([P, OUT], F32, tag="scaled", bufs=4)
            nc.vector.scalar_tensor_tensor(
                out=scaled[:], in0=mean_tiles[j]["mu_lin"][:], scalar=mean_tiles[j]["neg_mean"][:], in1=ln_g_rows,
                op0=ALU.add, op1=ALU.mult,
            )
            mean_tiles[j]["scaled"] = scaled

        def mean_deviation(j):
            squares = head_pool.tile([P, OUT], F32, tag="squares", bufs=1)
            square_sum = small.tile([P, 1], F32, tag="square_sum")
            nc.scalar.activation(
                out=squares[:], in_=mean_tiles[j]["mu_lin"][:], func=ACT.Square, bias=mean_tiles[j]["row_sum"][:],
                scale=-1.0 * OUT, accum_out=square_sum[:],
            )
            var_eps = small.tile([P, 1], F32, tag="var_eps")
            nc.gpsimd.tensor_scalar(
                out=var_eps[:], in0=square_sum[:], scalar1=1.0 / OUT**3, scalar2=LN_EPS, op0=ALU.mult, op1=ALU.add
            )
            rstd = small.tile([P, 1], F32, tag="rstd")
            nc.gpsimd.tensor_tensor(out=rstd[:], in0=var_eps[:], in1=neg_half[:], op=ALU.pow)
            mean_tiles[j]["rstd"] = rstd

        def mean_finish(j):
            scaled = mean_tiles[j]["scaled"]
            nc.vector.scalar_tensor_tensor(
                out=scaled[:], in0=scaled[:], scalar=mean_tiles[j]["rstd"][:], in1=ln_b_rows, op0=ALU.mult, op1=ALU.add
            )
            nc.sync.dma_start(out=mu_out[:, j, :], in_=scaled[:])

        def spread_sum(j):
            nc.vector.tensor_tensor(out=spread_in[:, j, :], in0=head_acc[(j, 1)][:], in1=sig_b_rows, op=ALU.add)

        def spread_sigmoid(tiles):
            nc.scalar.activation(out=spread_log[:, tiles, :], in_=spread_in[:, tiles, :], func=ACT.Sigmoid, scale=-1.0)

        def spread_ln(j):
            nc.scalar.activation(
                out=spread_log[:, j, :], in_=spread_log[:, j, :], func=ACT.Ln, bias=tiny[:], scale=math.exp(-SIG_MIN)
            )

        def spread_finish(j):
            nc.vector.scalar_tensor_tensor(
                out=spread_in[:, j, :], in0=spread_log[:, j, :], scalar=-1.0, in1=spread_in[:, j, :],
                op0=ALU.mult, op1=ALU.max,
            )
            nc.sync.dma_start(out=sigma_out[:, j, :], in_=spread_in[:, j, :])

        VECTOR, SCALAR = nc.vector.tensor_copy, nc.scalar.copy
        load_rows(0)
        load_vectors()
        for r in range(1, RAW_BUFS):
            load_rows(r)
        keep_warm(6)
        transpose_rows(0)
        keep_warm(2)
        load_rows(RAW_BUFS)
        for b in range(BANKS):
            empty_bank(0, b, SCALAR)
        quantise_banks(0, 0, 2)
        quantise_banks(0, 2, 2)
        turn_vectors()
        transpose_bank(1, 0)
        transpose_bank(1, 1)
        transpose_bank(1, 2)
        transpose_bank(1, 3)
        load_rows(1 + RAW_BUFS)
        for b in range(BANKS):
            empty_bank(1, b, SCALAR)
        quantise_banks(1, 0, 2)
        transpose_bank(2, 0)
        transpose_bank(2, 1)
        empty_bank(2, 0, VECTOR)
        quantise_banks(1, 2, 2)
        empty_bank(2, 1, VECTOR)
        gate_product(0, 0)
        gate_product(0, 1)
        transpose_bank(2, 2)
        transpose_bank(2, 3)
        gate_product(0, 2)
        gate_product(0, 3)
        load_rows(2 + RAW_BUFS)
        empty_bank(2, 2, VECTOR)
        quantise_banks(2, 0, 2)
        empty_bank(2, 3, VECTOR)
        quantise_banks(2, 2, 2)
        transpose_rows(3)
        load_rows(3 + RAW_BUFS)

        def piece(m):
            return m // PARTS[0], m % PARTS[0]

        HIDDEN_LAG = PACK + 1
        FIRST_HEAD = PARTS[0] + HIDDEN_LAG + 1
        HEADS0 = PARTS[0]
        for n in range(UNITS):
            r = n + 3
            m = n - HIDDEN_LAG
            j = n - FIRST_HEAD
            loading = r < len(sources)
            heads = 0 <= j < HEADS0
            if heads:
                head_product(j, 0)
                head_product(j, 1)
            if n > 0:
                cell_input(n - 1)
            if 3 < r <= len(sources):
                quantise_banks(r - 1, 2, 2)
            if m >= 0:
                hidden_product(*piece(m))
            if loading:
                empty_bank(r, 0, VECTOR)
            if loading:
                empty_bank(r, 1, VECTOR)
            if heads:
                mean_sum(j)
            if n > 0:
                cell_new(n - 1)
            if m >= 0:
                hidden_quantise(*piece(m))
            if 0 <= j - 1 < HEADS0:
                mean_finish(j - 1)
            if heads:
                mean_centre(j)
            if loading:
                quantise_banks(r, 0, 2)
            if heads:
                spread_sum(j)
            if heads:
                mean_scale(j)
            for q in range(GATES):
                gate(n, q)
            if loading:
                empty_bank(r, 2, SCALAR)
                empty_bank(r, 3, SCALAR)
            if n > 0:
                cell_tanh(n - 1)
            if heads:
                mean_deviation(j)
            if r + 1 < len(sources):
                transpose_rows(r + 1)
                if r + 1 + RAW_BUFS < len(sources):
                    load_rows(r + 1 + RAW_BUFS)

        first_left = UNITS - HIDDEN_LAG
        cell_input(UNITS - 1)
        keep_warm(0)
        hidden_product(*piece(first_left))
        keep_warm(2, hidden[piece(first_left)])
        cell_new(UNITS - 1)
        hidden_quantise(*piece(first_left))
        cell_tanh(UNITS - 1)
        spread_sigmoid(slice(0, HEADS0))
        for m in range(first_left + 1, 16):
            hidden_product(*piece(m))
            if m == first_left + 1:
                keep_warm(0, hidden[piece(m)])
            if m > first_left + 1:
                hidden_quantise(*piece(m - 1))
        late = range(HEADS0, B_TILES)
        for j in late:
            head_product(j, 0)
            if j == HEADS0:
                mean_sum(j)
                hidden_quantise(*piece(15))
            else:
                mean_sum(j)
            head_product(j, 1, *((psum_gates, "gate") if j >= 6 else ()))
            spread_sum(j)
            mean_centre(j)
            mean_deviation(j)
            spread_sigmoid(j)
        mean_scale(4)
        mean_scale(5)
        mean_finish(4)
        mean_scale(6)
        mean_finish(5)
        mean_scale(7)
        mean_finish(6)
        spread_ln(0)
        spread_finish(0)
        mean_finish(7)
        for j in range(1, B_TILES):
            spread_ln(j)
            spread_finish(j)
